import numpy as np
import ml_dtypes


def mxq(x, axis, fmt="e4m3"):
    dtype, down = {"e4m3": (ml_dtypes.float8_e4m3fn, 7), "e5m2": (ml_dtypes.float8_e5m2, 14)}[fmt]
    v = np.moveaxis(np.asarray(x, np.float32).astype(ml_dtypes.bfloat16).astype(np.float64), axis, -1)
    blocks = v.reshape(v.shape[:-1] + (-1, 32))
    amax = np.abs(blocks).max(-1, keepdims=True)
    byte = np.maximum(np.where(amax > 0, np.frexp(amax)[1] - 1 + 127, 0) - down, 1)
    scale = np.exp2(byte - 127.0)
    codes = (blocks / scale).astype(np.float32).astype(dtype).astype(np.float64)
    return np.moveaxis((codes * scale).reshape(v.shape), -1, axis)


WIDE = False


def mx_kscale(k):
    if not WIDE:
        return np.ones(k)
    levels = np.array([10, -10, 5, -5, 0])
    if k % 512:
        return np.exp2(np.random.permutation(np.resize(levels, k // 32))).repeat(32)
    a = np.empty((k // 512, 16))
    for p in range(k // 512):
        a[p, :8] = np.random.permutation(np.resize(levels, 8))
        for g in range(8):
            far = levels[np.abs(levels - a[p, g]) >= 10]
            a[p, g + 8] = far[np.random.randint(len(far))]
    return np.exp2(a.ravel()).repeat(32)


BF16 = ml_dtypes.bfloat16


def bf(x):
    return np.asarray(x, np.float32).astype(BF16)


def f64(x):
    return np.asarray(x).astype(np.float64)


B, C, HH, WW, HD = 1, 1024, 32, 32, 128
S = HH * WW
NH = C // HD
EPS = 1e-4


def mp_weight(w):
    o, i, kh, kw = w.shape
    fan_in = i * kh * kw
    n = np.sqrt(np.sum(w * w, axis=(1, 2, 3), keepdims=True))
    alpha = 1.0 / np.sqrt(fan_in)
    wn = w / (EPS + alpha * n) / np.sqrt(fan_in)
    return wn[:, :, 0, 0]


def pixel_norm(t):
    return t * (1.0 / np.sqrt(np.mean(t * t, axis=1, keepdims=True) + EPS))


def to_heads(t):
    return t.reshape(B, S, NH, HD).transpose(0, 2, 1, 3)


def setup_inputs():
    s = mx_kscale(C)
    sc = s * np.sqrt(np.mean(1.0 / s**2))
    gain = 0.002 * np.exp2(np.random.uniform(-2.0, 2.0, 3 * C))
    return {"x": bf(np.random.standard_normal((B, C, HH, WW)) * 0.06 * sc[None, :, None, None]),
            "w_attn": bf(np.random.standard_normal((3 * C, C, 1, 1)) * gain[:, None, None, None] / sc[None, :, None, None])}


def reference(x, w_attn):
    wn = mp_weight(f64(w_attn))
    xt = f64(x).reshape(B, C, S).transpose(0, 2, 1)
    p = mxq(xt, 2, "e4m3") @ mxq(wn.T, 0, "e4m3")
    q, k, v = np.split(p, 3, axis=-1)
    return pixel_norm(to_heads(q)), pixel_norm(to_heads(k)), pixel_norm(to_heads(v))

@@ -1,0 +1,282 @@
+import math
+from contextlib import ExitStack
+
+import concourse.masks as masks
+import concourse.mybir as mybir
+
+F32 = mybir.dt.float32
+BF16 = mybir.dt.bfloat16
+U32 = mybir.dt.uint32
+U8 = mybir.dt.uint8
+FP8X4 = mybir.dt.float8_e4m3fn_x4
+ACT = mybir.ActivationFunctionType
+ALU = mybir.AluOpType
+
+P = 128
+PACK = 4
+CHANNELS = 1024
+PASSES = CHANNELS // (P * PACK)
+POSITIONS = 1024
+HEADS = 8
+HEAD_DIM = 128
+THIRDS = 3
+EPS = 1e-4
+NORM_FLOOR = EPS * math.sqrt(CHANNELS)
+BANK = 512
+HEADS_PER_BANK = BANK // HEAD_DIM
+BANKS_PER_GROUP = HEADS // HEADS_PER_BANK
+
+BLOCKS = THIRDS * HEADS
+GROUPS_PER_THIRD = POSITIONS // P
+GROUPS = THIRDS * GROUPS_PER_THIRD
+X_COLUMNS = 512
+X_UNITS = PASSES * POSITIONS // X_COLUMNS
+
+FLOPS = 2 * POSITIONS * CHANNELS * THIRDS * HEADS * HEAD_DIM
+
+
+def tile_cosineattention_pa_kernel(tc, x, w_attn, out_0, out_1, out_2):
+    nc = tc.nc
+    x_rows = x.rearrange("b c h w -> (b c) (h w)")
+    w_rows = w_attn.rearrange("o i a b -> o (i a b)")
+    outs = [o.rearrange("b n s d -> (b n) s d") for o in (out_0, out_1, out_2)]
+
+    with ExitStack() as ctx:
+        ctx.enter_context(tc.manual_schedule())
+        keep = ctx.enter_context(tc.tile_pool(name="keep", bufs=1))
+        x_stage = ctx.enter_context(tc.tile_pool(name="x_stage", bufs=2))
+        w_stage = ctx.enter_context(tc.tile_pool(name="w_stage", bufs=3))
+        tiny = ctx.enter_context(tc.tile_pool(name="tiny", bufs=3))
+        norm = ctx.enter_context(tc.tile_pool(name="norm", bufs=3))
+        results = ctx.enter_context(tc.tile_pool(name="results", bufs=6))
+        psum = ctx.enter_context(tc.psum_pool(name="psum", bufs=2))
+
+        identity = keep.tile([P, P], F32)
+        zero_column = keep.tile([P, 1], F32)
+        eps_column = keep.tile([P, 1], F32)
+        table_warmer = keep.tile([P, 1], F32)
+        half_pair = keep.tile([P, 2], F32)
+        minus_one_pair = keep.tile([P, 2], F32)
+        x_raw = keep.tile([P, PASSES * PACK, POSITIONS], BF16)
+        x_codes = keep.tile([P, PASSES, POSITIONS], U32, align_bytes=64)
+        x_scales = keep.tile([P, PASSES, POSITIONS], U8, align_bytes=64)
+        w_raw = keep.tile([P, BLOCKS, CHANNELS], BF16)
+        w_codes = keep.tile([P, BLOCKS // HEADS_PER_BANK, PASSES, BANK], U32, align_bytes=64)
+        w_scales = keep.tile([P, BLOCKS // HEADS_PER_BANK, PASSES, BANK], U8, align_bytes=64)
+
+        sum_squares = {}
+        filter_scales = {}
+        normed = {}
+        turned = {}
+        grouped_w = {}
+        grouped_x = {}
+        products = {}
+        squares = {}
+        folded_squares = {}
+        head_sums = {}
+        inv_rms = {}
+
+        def load_everything():
+            for b in range(BLOCKS):
+                nc.sync.dma_start(out=w_raw[:, b, :], in_=w_rows[P * b : P * (b + 1), :])
+                if b < PASSES * 2:
+                    g, u = divmod(b, 2)
+                    nc.sync.dma_start(
+                        out=x_raw[:, 2 * b : 2 * b + 2, :],
+                        in_=x_rows[PACK * P * g : PACK * P * (g + 1), :].rearrange("(p t) s -> p t s", t=PACK)[
+                            :, 2 * u : 2 * u + 2, :
+                        ],
+                    )
+
+        def regroup_x(unit):
+            g, part = divmod(unit, POSITIONS // X_COLUMNS)
+            grouped = x_stage.tile([P, X_COLUMNS, PACK], BF16, align_bytes=64)
+            nc.vector.tensor_copy(
+                out=grouped[:],
+                in_=x_raw[:, PACK * g : PACK * (g + 1), X_COLUMNS * part : X_COLUMNS * (part + 1)].rearrange(
+                    "p t s -> p s t"
+                ),
+            )
+            grouped_x[unit] = grouped
+
+        def quantise_x(unit):
+            g, part = divmod(unit, POSITIONS // X_COLUMNS)
+            columns = slice(X_COLUMNS * part, X_COLUMNS * (part + 1))
+            nc.vector.quantize_mx(
+                out=x_codes[:, g, columns].bitcast(FP8X4),
+                scales=x_scales[:, g, columns],
+                in_=grouped_x[unit][:].rearrange("p s t -> p (s t)"),
+            )
+
+        def filter_sum_squares(b):
+            pair, member = divmod(b, 2)
+            if member == 0:
+                sum_squares[pair] = tiny.tile([P, 2], F32, name="totals")
+            unread = w_stage.tile([P, CHANNELS], BF16)
+            nc.scalar.activation(
+                out=unread[:], in_=w_raw[:, b, :], func=ACT.Square, accum_out=sum_squares[pair][:, member : member + 1]
+            )
+
+        def filter_scale(pair):
+            lengths = tiny.tile([P, 2], F32)
+            nc.gpsimd.tensor_tensor(out=lengths[:], in0=sum_squares[pair][:], in1=half_pair[:], op=ALU.pow)
+            padded = tiny.tile([P, 2], F32)
+            nc.gpsimd.tensor_scalar_add(out=padded[:], in0=lengths[:], scalar1=NORM_FLOOR)
+            scales = tiny.tile([P, 2], F32)
+            nc.gpsimd.tensor_tensor(out=scales[:], in0=padded[:], in1=minus_one_pair[:], op=ALU.pow)
+            filter_scales[pair] = scales
+
+        def normalise_filters(b):
+            pair, member = divmod(b, 2)
+            wn = w_stage.tile([P, CHANNELS], BF16)
+            nc.vector.tensor_scalar_mul(
+                out=wn[:], in0=w_raw[:, b, :], scalar1=filter_scales[pair][:, member : member + 1]
+            )
+            normed[b] = wn
+
+        def transpose_filters(b):
+            words = normed[b][:].bitcast(F32)
+            bank = psum.tile([P, PASSES * 2, P], F32, tag="turned", bufs=1)
+            for c in range(PASSES * 2):
+                g, u = divmod(c, 2)
+                nc.tensor.transpose(bank[:, c, :], words[:, 2 * P * g + u : 2 * P * (g + 1) : 2], identity[:])
+            turned[b] = bank
+
+        def regroup_filters(b):
+            grouped = w_stage.tile([P, PASSES, P, PACK], BF16, align_bytes=64)
+            copy = nc.scalar.copy if b < HEADS or b % 2 == 1 else nc.vector.tensor_copy
+            copy(
+                out=grouped[:]
+                .rearrange("p g o t -> p (g o t)")
+                .bitcast(F32)
+                .rearrange("p (g o u) -> p g o u", g=PASSES, u=2),
+                in_=turned[b][:].rearrange("p (g u) o -> p g o u", u=2),
+            )
+            grouped_w[b] = grouped
+
+        def quantise_filters(b):
+            bank, head = divmod(b, HEADS_PER_BANK)
+            columns = slice(HEAD_DIM * head, HEAD_DIM * (head + 1))
+            for g in range(PASSES):
+                nc.vector.quantize_mx(
+                    out=w_codes[:, bank, g, columns].bitcast(FP8X4),
+                    scales=w_scales[:, bank, g, columns],
+                    in_=grouped_w[b][:, g].rearrange("p o t -> p (o t)"),
+                )
+
+        def project(q):
+            third, block = divmod(q, GROUPS_PER_THIRD)
+            columns = slice(P * block, P * (block + 1))
+            banks = []
+            for h in range(BANKS_PER_GROUP):
+                bank = psum.tile([P, BANK], F32, tag="product", bufs=6)
+                for g in range(PASSES):
+                    nc.tensor.matmul_mx(
+                        out=bank[:],
+                        lhsT=x_codes[:, g, columns].bitcast(FP8X4),
+                        lhsT_scale=x_scales[:, g, columns],
+                        rhs=w_codes[:, BANKS_PER_GROUP * third + h, g, :].bitcast(FP8X4),
+                        rhs_scale=w_scales[:, BANKS_PER_GROUP * third + h, g, :],
+                        start=(g == 0),
+                        stop=(g == PASSES - 1),
+                    )
+                banks.append(bank)
+            products[q] = banks
+
+        def square_products(q):
+            sq = norm.tile([P, HEADS * HEAD_DIM], F32)
+            for h in range(BANKS_PER_GROUP):
+                nc.scalar.activation(out=sq[:, BANK * h : BANK * (h + 1)], in_=products[q][h][:], func=ACT.Square)
+            squares[q] = sq
+
+        def fold_heads(q):
+            folded = norm.tile([P, BANK], F32)
+            nc.vector.tensor_tensor(out=folded[:], in0=squares[q][:, :BANK], in1=squares[q][:, BANK:], op=ALU.add)
+            folded_squares[q] = folded
+
+        def add_folded_heads(q):
+            total = psum.tile([P, HEAD_DIM], F32, tag="head_sum", bufs=1)
+            for n in range(HEADS_PER_BANK):
+                nc.tensor.matmul(
+                    out=total[:],
+                    lhsT=identity[:],
+                    rhs=folded_squares[q][:, HEAD_DIM * n : HEAD_DIM * (n + 1)],
+                    start=(n == 0),
+                    stop=(n == HEADS_PER_BANK - 1),
+                )
+            head_sums[q] = total
+
+        def inverse_rms(q):
+            r = norm.tile([P, HEAD_DIM], F32)
+            nc.scalar.activation(
+                out=r[:], in_=head_sums[q][:], func=ACT.Abs_reciprocal_sqrt, scale=1.0 / HEADS, bias=eps_column[:]
+            )
+            inv_rms[q] = r
+
+        def scale_and_store(q, h):
+            third, block = divmod(q, GROUPS_PER_THIRD)
+            heads = slice(HEADS_PER_BANK * h, HEADS_PER_BANK * (h + 1))
+            res = results.tile([P, HEADS_PER_BANK, HEAD_DIM], F32)
+            nc.vector.tensor_tensor(
+                out=res[:],
+                in0=products[q][h][:].rearrange("p (n d) -> p n d", n=HEADS_PER_BANK),
+                in1=inv_rms[q][:].unsqueeze(1).to_broadcast([P, HEADS_PER_BANK, HEAD_DIM]),
+                op=ALU.mult,
+            )
+            nc.sync.dma_start(
+                out=outs[third][heads, P * block : P * (block + 1), :].rearrange("n s d -> s n d"), in_=res[:]
+            )
+
+        load_everything()
+        nc.vector.memset(zero_column[:], 0.0)
+        nc.vector.tensor_scalar_add(out=eps_column[:], in0=zero_column[:], scalar1=EPS)
+        nc.vector.memset(half_pair[:], 0.5)
+        nc.vector.memset(minus_one_pair[:], -1.0)
+        nc.scalar.activation(out=table_warmer[:], in_=eps_column[:], func=ACT.Abs_reciprocal_sqrt)
+        masks.make_identity(nc, identity[:])
+
+        def is_block(b):
+            return 0 <= b < BLOCKS
+
+        def is_group(q):
+            return 0 <= q < GROUPS
+
+        last_block_stage = 4
+        first_product_step = HEADS - 1 + last_block_stage
+        last_group_stage = 3
+        for step in range(first_product_step + GROUPS + last_group_stage):
+            summed, scaled, moved, coded = step, step - 2, step - 3, step - last_block_stage
+            made = step - first_product_step
+            squared, added, stored = made - 1, made - 2, made - last_group_stage
+
+            if is_group(added):
+                fold_heads(added)
+            if is_group(stored):
+                for h in range(BANKS_PER_GROUP):
+                    scale_and_store(stored, h)
+            if is_block(coded):
+                quantise_filters(coded)
+            if is_block(moved):
+                transpose_filters(moved)
+            if is_group(added):
+                add_folded_heads(added)
+            if is_block(summed):
+                filter_sum_squares(summed)
+                if summed % 2 == 1:
+                    filter_scale(summed // 2)
+            if is_group(squared):
+                square_products(squared)
+            if is_group(added):
+                inverse_rms(added)
+            if is_block(moved):
+                regroup_filters(moved)
+            if is_block(scaled):
+                normalise_filters(scaled)
+            if is_group(made):
+                project(made)
+            unit, quantise = divmod(step - 2, 2)
+            if 0 <= unit < X_UNITS:
+                if quantise:
+                    quantise_x(unit)
+                else:
+                    regroup_x(unit)

@@ -128,18 +128,21 @@ def tile_cosineattention_pa_kernel(tc, x, w_attn, out_0, out_1, out_2):
 
         def normalise_filters(b):
             pair, member = divmod(b, 2)
-            wn = w_stage.tile([P, CHANNELS], BF16)
+            wn = w_stage.tile([P, 2, CHANNELS // PACK, 2], BF16)
             nc.vector.tensor_scalar_mul(
-                out=wn[:], in0=w_raw[:, b, :], scalar1=filter_scales[pair][:, member : member + 1]
+                out=wn[:],
+                in0=w_raw[:, b, :].rearrange("o (r u e) -> o u r e", u=2, e=2),
+                scalar1=filter_scales[pair][:, member : member + 1],
             )
             normed[b] = wn
 
         def transpose_filters(b):
-            words = normed[b][:].bitcast(F32)
+            words = normed[b][:].rearrange("o u r e -> o (u r e)").bitcast(F32)
             bank = psum.tile([P, PASSES * 2, P], F32, tag="turned", bufs=1)
             for c in range(PASSES * 2):
                 g, u = divmod(c, 2)
-                nc.tensor.transpose(bank[:, c, :], words[:, 2 * P * g + u : 2 * P * (g + 1) : 2], identity[:])
+                start = P * (PASSES * u + g)
+                nc.tensor.transpose(bank[:, c, :], words[:, start : start + P], identity[:])
             turned[b] = bank
 
         def regroup_filters(b):

@@ -55,8 +55,7 @@ def tile_cosineattention_pa_kernel(tc, x, w_attn, out_0, out_1, out_2):
         zero_column = keep.tile([P, 1], F32)
         eps_column = keep.tile([P, 1], F32)
         table_warmer = keep.tile([P, 1], F32)
-        half_pair = keep.tile([P, 2], F32)
-        minus_one_pair = keep.tile([P, 2], F32)
+        tiny_column = keep.tile([P, 1], F32)
         x_raw = keep.tile([P, PASSES * PACK, POSITIONS], BF16)
         x_codes = keep.tile([P, PASSES, POSITIONS], U32, align_bytes=64)
         x_scales = keep.tile([P, PASSES, POSITIONS], U8, align_bytes=64)
@@ -65,6 +64,9 @@ def tile_cosineattention_pa_kernel(tc, x, w_attn, out_0, out_1, out_2):
         w_scales = keep.tile([P, BLOCKS // HEADS_PER_BANK, PASSES, BANK], U8, align_bytes=64)
 
         sum_squares = {}
+        inverse_lengths = {}
+        lengths = {}
+        padded_lengths = {}
         filter_scales = {}
         normed = {}
         turned = {}
@@ -117,13 +119,28 @@ def tile_cosineattention_pa_kernel(tc, x, w_attn, out_0, out_1, out_2):
                 out=unread[:], in_=w_raw[:, b, :], func=ACT.Square, accum_out=sum_squares[pair][:, member : member + 1]
             )
 
-        def filter_scale(pair):
-            lengths = tiny.tile([P, 2], F32)
-            nc.gpsimd.tensor_tensor(out=lengths[:], in0=sum_squares[pair][:], in1=half_pair[:], op=ALU.pow)
+        def filter_inverse_length(pair):
+            inverse = tiny.tile([P, 2], F32)
+            nc.scalar.activation(
+                out=inverse[:], in_=sum_squares[pair][:], func=ACT.Abs_reciprocal_sqrt, bias=tiny_column[:]
+            )
+            inverse_lengths[pair] = inverse
+
+        def filter_length(pair):
+            length = tiny.tile([P, 2], F32)
+            nc.vector.tensor_tensor(
+                out=length[:], in0=sum_squares[pair][:], in1=inverse_lengths[pair][:], op=ALU.mult
+            )
+            lengths[pair] = length
+
+        def filter_floor(pair):
             padded = tiny.tile([P, 2], F32)
-            nc.gpsimd.tensor_scalar_add(out=padded[:], in0=lengths[:], scalar1=NORM_FLOOR)
+            nc.vector.tensor_scalar_add(out=padded[:], in0=lengths[pair][:], scalar1=NORM_FLOOR)
+            padded_lengths[pair] = padded
+
+        def filter_scale(pair):
             scales = tiny.tile([P, 2], F32)
-            nc.gpsimd.tensor_tensor(out=scales[:], in0=padded[:], in1=minus_one_pair[:], op=ALU.pow)
+            nc.vector.reciprocal(out=scales[:], in_=padded_lengths[pair][:])
             filter_scales[pair] = scales
 
         def normalise_filters(b):
@@ -233,8 +250,7 @@ def tile_cosineattention_pa_kernel(tc, x, w_attn, out_0, out_1, out_2):
         load_everything()
         nc.vector.memset(zero_column[:], 0.0)
         nc.vector.tensor_scalar_add(out=eps_column[:], in0=zero_column[:], scalar1=EPS)
-        nc.vector.memset(half_pair[:], 0.5)
-        nc.vector.memset(minus_one_pair[:], -1.0)
+        nc.vector.tensor_scalar_add(out=tiny_column[:], in0=zero_column[:], scalar1=1e-30)
         nc.scalar.activation(out=table_warmer[:], in_=eps_column[:], func=ACT.Abs_reciprocal_sqrt)
         masks.make_identity(nc, identity[:])
 
@@ -244,29 +260,34 @@ def tile_cosineattention_pa_kernel(tc, x, w_attn, out_0, out_1, out_2):
         def is_group(q):
             return 0 <= q < GROUPS
 
-        last_block_stage = 4
+        last_block_stage = 5
         first_product_step = HEADS - 1 + last_block_stage
         last_group_stage = 3
         for step in range(first_product_step + GROUPS + last_group_stage):
-            summed, scaled, moved, coded = step, step - 2, step - 3, step - last_block_stage
+            summed, scaled, moved, coded = step, step - 3, step - 4, step - last_block_stage
+            pair = (step - 2) // 2 if step % 2 == 0 and 0 < step <= BLOCKS else None
             made = step - first_product_step
             squared, added, stored = made - 1, made - 2, made - last_group_stage
 
+            if pair is not None:
+                filter_inverse_length(pair)
             if is_group(added):
                 fold_heads(added)
             if is_group(stored):
                 for h in range(BANKS_PER_GROUP):
                     scale_and_store(stored, h)
+            if pair is not None:
+                filter_length(pair)
             if is_block(coded):
                 quantise_filters(coded)
+            if pair is not None:
+                filter_floor(pair)
             if is_block(moved):
                 transpose_filters(moved)
             if is_group(added):
                 add_folded_heads(added)
             if is_block(summed):
                 filter_sum_squares(summed)
-                if summed % 2 == 1:
-                    filter_scale(summed // 2)
             if is_group(squared):
                 square_products(squared)
             if is_group(added):
@@ -275,6 +296,8 @@ def tile_cosineattention_pa_kernel(tc, x, w_attn, out_0, out_1, out_2):
                 regroup_filters(moved)
             if is_block(scaled):
                 normalise_filters(scaled)
+            if pair is not None:
+                filter_scale(pair)
             if is_group(made):
                 project(made)
             unit, quantise = divmod(step - 2, 2)

@@ -23,14 +23,17 @@ THIRDS = 3
 EPS = 1e-4
 NORM_FLOOR = EPS * math.sqrt(CHANNELS)
 BANK = 512
-HEADS_PER_BANK = BANK // HEAD_DIM
-BANKS_PER_GROUP = HEADS // HEADS_PER_BANK
 
-BLOCKS = THIRDS * HEADS
-GROUPS_PER_THIRD = POSITIONS // P
-GROUPS = THIRDS * GROUPS_PER_THIRD
-X_COLUMNS = 512
-X_UNITS = PASSES * POSITIONS // X_COLUMNS
+HALF = HEAD_DIM // 2
+PHASES = 2 * THIRDS
+BLOCKS_PER_PHASE = HEADS // 2
+BLOCKS = PHASES * BLOCKS_PER_PHASE
+BANKS_PER_GROUP = 2
+GROUP_POSITIONS = BANKS_PER_GROUP * P
+GROUPS_PER_PHASE = POSITIONS // GROUP_POSITIONS
+GROUPS = PHASES * GROUPS_PER_PHASE
+X_UNITS = PASSES * GROUPS_PER_PHASE
+FIRST_VECTOR_FOLD = 20
 
 FLOPS = 2 * POSITIONS * CHANNELS * THIRDS * HEADS * HEAD_DIM
 
@@ -38,13 +41,13 @@ FLOPS = 2 * POSITIONS * CHANNELS * THIRDS * HEADS * HEAD_DIM
 def tile_cosineattention_pa_kernel(tc, x, w_attn, out_0, out_1, out_2):
     nc = tc.nc
     x_rows = x.rearrange("b c h w -> (b c) (h w)")
-    w_rows = w_attn.rearrange("o i a b -> o (i a b)")
+    w_halves = w_attn.rearrange("(t j i h d) c a b -> t h i d j (c a b)", t=THIRDS, i=2, h=2, d=HALF)
     outs = [o.rearrange("b n s d -> (b n) s d") for o in (out_0, out_1, out_2)]
 
     with ExitStack() as ctx:
         ctx.enter_context(tc.manual_schedule())
         keep = ctx.enter_context(tc.tile_pool(name="keep", bufs=1))
-        x_stage = ctx.enter_context(tc.tile_pool(name="x_stage", bufs=2))
+        x_stage = ctx.enter_context(tc.tile_pool(name="x_stage", bufs=3))
         w_stage = ctx.enter_context(tc.tile_pool(name="w_stage", bufs=3))
         tiny = ctx.enter_context(tc.tile_pool(name="tiny", bufs=3))
         norm = ctx.enter_context(tc.tile_pool(name="norm", bufs=3))
@@ -56,12 +59,13 @@ def tile_cosineattention_pa_kernel(tc, x, w_attn, out_0, out_1, out_2):
         eps_column = keep.tile([P, 1], F32)
         table_warmer = keep.tile([P, 1], F32)
         tiny_column = keep.tile([P, 1], F32)
-        x_raw = keep.tile([P, PASSES * PACK, POSITIONS], BF16)
+        x_early = keep.tile([P, PASSES * PACK, GROUP_POSITIONS], BF16)
+        x_late = keep.tile([P, PASSES * PACK, POSITIONS - GROUP_POSITIONS], BF16)
         x_codes = keep.tile([P, PASSES, POSITIONS], U32, align_bytes=64)
         x_scales = keep.tile([P, PASSES, POSITIONS], U8, align_bytes=64)
         w_raw = keep.tile([P, BLOCKS, CHANNELS], BF16)
-        w_codes = keep.tile([P, BLOCKS // HEADS_PER_BANK, PASSES, BANK], U32, align_bytes=64)
-        w_scales = keep.tile([P, BLOCKS // HEADS_PER_BANK, PASSES, BANK], U8, align_bytes=64)
+        w_codes = keep.tile([P, PHASES, PASSES, BANK], U32, align_bytes=64)
+        w_scales = keep.tile([P, PHASES, PASSES, BANK], U8, align_bytes=64)
 
         sum_squares = {}
         inverse_lengths = {}
@@ -77,37 +81,55 @@ def tile_cosineattention_pa_kernel(tc, x, w_attn, out_0, out_1, out_2):
         folded_squares = {}
         head_sums = {}
         inv_rms = {}
+        finished = {}
+
+        def load_x(g, early):
+            rows = x_rows[PACK * P * g : PACK * P * (g + 1), :].rearrange("(p t) s -> p t s", t=PACK)
+            nc.sync.dma_start(
+                out=(x_early if early else x_late)[:, PACK * g : PACK * (g + 1), :],
+                in_=rows[:, :, :GROUP_POSITIONS] if early else rows[:, :, GROUP_POSITIONS:],
+            )
+
+        def load_filters(phase, first, last):
+            third, half = divmod(phase, 2)
+            blocks = slice(BLOCKS_PER_PHASE * phase + first, BLOCKS_PER_PHASE * phase + last)
+            for i in range(2):
+                nc.sync.dma_start(
+                    out=w_raw[HALF * i : HALF * (i + 1), blocks, :], in_=w_halves[third, half, i, :, first:last, :]
+                )
 
         def load_everything():
-            for b in range(BLOCKS):
-                nc.sync.dma_start(out=w_raw[:, b, :], in_=w_rows[P * b : P * (b + 1), :])
-                if b < PASSES * 2:
-                    g, u = divmod(b, 2)
-                    nc.sync.dma_start(
-                        out=x_raw[:, 2 * b : 2 * b + 2, :],
-                        in_=x_rows[PACK * P * g : PACK * P * (g + 1), :].rearrange("(p t) s -> p t s", t=PACK)[
-                            :, 2 * u : 2 * u + 2, :
-                        ],
-                    )
+            for j in range(BLOCKS_PER_PHASE):
+                load_filters(0, j, j + 1)
+                if j < PASSES:
+                    load_x(j, True)
+            load_filters(1, 0, 2)
+            load_filters(1, 2, 4)
+            for g in range(PASSES):
+                load_x(g, False)
+            for phase in range(2, PHASES):
+                load_filters(phase, 0, BLOCKS_PER_PHASE)
 
         def regroup_x(unit):
-            g, part = divmod(unit, POSITIONS // X_COLUMNS)
-            grouped = x_stage.tile([P, X_COLUMNS, PACK], BF16, align_bytes=64)
+            k, g = divmod(unit, PASSES)
+            grouped = x_stage.tile([P, BANKS_PER_GROUP, P, PACK], BF16, align_bytes=64)
+            channels = slice(PACK * g, PACK * (g + 1))
+            if k == 0:
+                rows = x_early[:, channels, :]
+            else:
+                rows = x_late[:, channels, GROUP_POSITIONS * (k - 1) : GROUP_POSITIONS * k]
             nc.vector.tensor_copy(
-                out=grouped[:],
-                in_=x_raw[:, PACK * g : PACK * (g + 1), X_COLUMNS * part : X_COLUMNS * (part + 1)].rearrange(
-                    "p t s -> p s t"
-                ),
+                out=grouped[:], in_=rows.rearrange("p t (s j) -> p j s t", j=BANKS_PER_GROUP)
             )
             grouped_x[unit] = grouped
 
         def quantise_x(unit):
-            g, part = divmod(unit, POSITIONS // X_COLUMNS)
-            columns = slice(X_COLUMNS * part, X_COLUMNS * (part + 1))
+            k, g = divmod(unit, PASSES)
+            columns = slice(GROUP_POSITIONS * k, GROUP_POSITIONS * (k + 1))
             nc.vector.quantize_mx(
                 out=x_codes[:, g, columns].bitcast(FP8X4),
                 scales=x_scales[:, g, columns],
-                in_=grouped_x[unit][:].rearrange("p s t -> p (s t)"),
+                in_=grouped_x[unit][:].rearrange("p j s t -> p (j s t)"),
             )
 
         def filter_sum_squares(b):
@@ -155,7 +177,10 @@ def tile_cosineattention_pa_kernel(tc, x, w_attn, out_0, out_1, out_2):
 
         def transpose_filters(b):
             words = normed[b][:].rearrange("o u r e -> o (u r e)").bitcast(F32)
-            bank = psum.tile([P, PASSES * 2, P], F32, tag="turned", bufs=1)
+            first = b < BLOCKS_PER_PHASE
+            bank = psum.tile(
+                [P, PASSES * 2, P], F32, tag="product" if first else "turned", bufs=6 if first else 1
+            )
             for c in range(PASSES * 2):
                 g, u = divmod(c, 2)
                 start = P * (PASSES * u + g)
@@ -164,7 +189,7 @@ def tile_cosineattention_pa_kernel(tc, x, w_attn, out_0, out_1, out_2):
 
         def regroup_filters(b):
             grouped = w_stage.tile([P, PASSES, P, PACK], BF16, align_bytes=64)
-            copy = nc.scalar.copy if b < HEADS or b % 2 == 1 else nc.vector.tensor_copy
+            copy = nc.scalar.copy if b == BLOCKS_PER_PHASE - 1 else nc.vector.tensor_copy
             copy(
                 out=grouped[:]
                 .rearrange("p g o t -> p (g o t)")
@@ -175,28 +200,28 @@ def tile_cosineattention_pa_kernel(tc, x, w_attn, out_0, out_1, out_2):
             grouped_w[b] = grouped
 
         def quantise_filters(b):
-            bank, head = divmod(b, HEADS_PER_BANK)
-            columns = slice(HEAD_DIM * head, HEAD_DIM * (head + 1))
+            phase, j = divmod(b, BLOCKS_PER_PHASE)
+            columns = slice(P * j, P * (j + 1))
             for g in range(PASSES):
                 nc.vector.quantize_mx(
-                    out=w_codes[:, bank, g, columns].bitcast(FP8X4),
-                    scales=w_scales[:, bank, g, columns],
+                    out=w_codes[:, phase, g, columns].bitcast(FP8X4),
+                    scales=w_scales[:, phase, g, columns],
                     in_=grouped_w[b][:, g].rearrange("p o t -> p (o t)"),
                 )
 
         def project(q):
-            third, block = divmod(q, GROUPS_PER_THIRD)
-            columns = slice(P * block, P * (block + 1))
+            phase, k = divmod(q, GROUPS_PER_PHASE)
             banks = []
-            for h in range(BANKS_PER_GROUP):
-                bank = psum.tile([P, BANK], F32, tag="product", bufs=6)
+            for j in range(BANKS_PER_GROUP):
+                columns = slice(GROUP_POSITIONS * k + P * j, GROUP_POSITIONS * k + P * (j + 1))
+                bank = psum.tile([P, HEADS, HALF], F32, tag="product", bufs=6)
                 for g in range(PASSES):
                     nc.tensor.matmul_mx(
-                        out=bank[:],
+                        out=bank[:].rearrange("p n d -> p (n d)"),
                         lhsT=x_codes[:, g, columns].bitcast(FP8X4),
                         lhsT_scale=x_scales[:, g, columns],
-                        rhs=w_codes[:, BANKS_PER_GROUP * third + h, g, :].bitcast(FP8X4),
-                        rhs_scale=w_scales[:, BANKS_PER_GROUP * third + h, g, :],
+                        rhs=w_codes[:, phase, g, :].bitcast(FP8X4),
+                        rhs_scale=w_scales[:, phase, g, :],
                         start=(g == 0),
                         stop=(g == PASSES - 1),
                     )
@@ -204,48 +229,67 @@ def tile_cosineattention_pa_kernel(tc, x, w_attn, out_0, out_1, out_2):
             products[q] = banks
 
         def square_products(q):
-            sq = norm.tile([P, HEADS * HEAD_DIM], F32)
-            for h in range(BANKS_PER_GROUP):
-                nc.scalar.activation(out=sq[:, BANK * h : BANK * (h + 1)], in_=products[q][h][:], func=ACT.Square)
+            sq = norm.tile([P, BANKS_PER_GROUP, HEADS, HALF], F32)
+            for j in range(BANKS_PER_GROUP):
+                nc.scalar.activation(out=sq[:, j], in_=products[q][j][:], func=ACT.Square)
             squares[q] = sq
 
         def fold_heads(q):
-            folded = norm.tile([P, BANK], F32)
-            nc.vector.tensor_tensor(out=folded[:], in0=squares[q][:, :BANK], in1=squares[q][:, BANK:], op=ALU.add)
+            folded = norm.tile([P, HEADS // 2, BANKS_PER_GROUP, HALF], F32)
+            engine = nc.gpsimd if q < FIRST_VECTOR_FOLD else nc.vector
+            engine.tensor_tensor(
+                out=folded[:].rearrange("p n j d -> p j n d"),
+                in0=squares[q][:, :, : HEADS // 2, :],
+                in1=squares[q][:, :, HEADS // 2 :, :],
+                op=ALU.add,
+            )
             folded_squares[q] = folded
 
         def add_folded_heads(q):
-            total = psum.tile([P, HEAD_DIM], F32, tag="head_sum", bufs=1)
-            for n in range(HEADS_PER_BANK):
+            total = psum.tile([P, BANKS_PER_GROUP * HALF], F32, tag="head_sum", bufs=1)
+            for n in range(HEADS // 2):
                 nc.tensor.matmul(
                     out=total[:],
                     lhsT=identity[:],
-                    rhs=folded_squares[q][:, HEAD_DIM * n : HEAD_DIM * (n + 1)],
+                    rhs=folded_squares[q][:, n].rearrange("p j d -> p (j d)"),
                     start=(n == 0),
-                    stop=(n == HEADS_PER_BANK - 1),
+                    stop=(n == HEADS // 2 - 1),
                 )
             head_sums[q] = total
 
         def inverse_rms(q):
-            r = norm.tile([P, HEAD_DIM], F32)
+            r = norm.tile([P, BANKS_PER_GROUP, HALF], F32)
             nc.scalar.activation(
-                out=r[:], in_=head_sums[q][:], func=ACT.Abs_reciprocal_sqrt, scale=1.0 / HEADS, bias=eps_column[:]
+                out=r[:].rearrange("p j d -> p (j d)"),
+                in_=head_sums[q][:],
+                func=ACT.Abs_reciprocal_sqrt,
+                scale=1.0 / HEADS,
+                bias=eps_column[:],
             )
             inv_rms[q] = r
 
-        def scale_and_store(q, h):
-            third, block = divmod(q, GROUPS_PER_THIRD)
-            heads = slice(HEADS_PER_BANK * h, HEADS_PER_BANK * (h + 1))
-            res = results.tile([P, HEADS_PER_BANK, HEAD_DIM], F32)
-            nc.vector.tensor_tensor(
-                out=res[:],
-                in0=products[q][h][:].rearrange("p (n d) -> p n d", n=HEADS_PER_BANK),
-                in1=inv_rms[q][:].unsqueeze(1).to_broadcast([P, HEADS_PER_BANK, HEAD_DIM]),
-                op=ALU.mult,
-            )
-            nc.sync.dma_start(
-                out=outs[third][heads, P * block : P * (block + 1), :].rearrange("n s d -> s n d"), in_=res[:]
-            )
+        def scale_products(q):
+            phase, k = divmod(q, GROUPS_PER_PHASE)
+            third, half = divmod(phase, 2)
+            if half == 0:
+                finished[third, k] = results.tile([P, HEADS, BANKS_PER_GROUP, HEAD_DIM], F32, name="res")
+            res = finished[third, k]
+            for j in range(BANKS_PER_GROUP):
+                nc.vector.tensor_tensor(
+                    out=res[:, :, j, HALF * half : HALF * (half + 1)],
+                    in0=products[q][j][:],
+                    in1=inv_rms[q][:, j].unsqueeze(1).to_broadcast([P, HEADS, HALF]),
+                    op=ALU.mult,
+                )
+            if half == 1:
+                positions = slice(GROUP_POSITIONS * k, GROUP_POSITIONS * (k + 1))
+                for n in range(0, HEADS, HEADS // 2):
+                    nc.sync.dma_start(
+                        out=outs[third][n : n + HEADS // 2, positions, :].rearrange(
+                            "n (p j) d -> p n (j d)", j=BANKS_PER_GROUP
+                        ),
+                        in_=res[:, n : n + HEADS // 2].rearrange("p n j d -> p n (j d)"),
+                    )
 
         load_everything()
         nc.vector.memset(zero_column[:], 0.0)
@@ -254,55 +298,92 @@ def tile_cosineattention_pa_kernel(tc, x, w_attn, out_0, out_1, out_2):
         nc.scalar.activation(out=table_warmer[:], in_=eps_column[:], func=ACT.Abs_reciprocal_sqrt)
         masks.make_identity(nc, identity[:])
 
-        def is_block(b):
-            return 0 <= b < BLOCKS
+        pairs_ahead = BLOCKS_PER_PHASE // 2
+        for pair in range(pairs_ahead + 1):
+            a, b = 2 * pair, 2 * pair + 1
+            turning = pair < pairs_ahead
+            filter_sum_squares(a)
+            filter_sum_squares(b)
+            filter_inverse_length(pair)
+            if pair == 0:
+                regroup_x(0)
+                regroup_x(1)
+                filter_length(pair)
+                quantise_x(0)
+                filter_floor(pair)
+                quantise_x(1)
+                filter_scale(pair)
+                normalise_filters(a)
+                transpose_filters(a)
+                normalise_filters(b)
+                transpose_filters(b)
+                continue
+            filter_length(pair)
+            regroup_filters(a - 2)
+            filter_floor(pair)
+            if pair > 1:
+                quantise_filters(a - 3)
+            filter_scale(pair)
+            regroup_filters(a - 1)
+            normalise_filters(a)
+            if turning:
+                transpose_filters(a)
+            quantise_filters(a - 2)
+            normalise_filters(b)
+            if turning:
+                transpose_filters(b)
+        filter_sum_squares(6)
+        filter_sum_squares(7)
+        filter_inverse_length(3)
+        quantise_filters(3)
+        project(0)
+        transpose_filters(4)
+        regroup_x(2)
+        regroup_x(3)
+        filter_length(3)
+        regroup_filters(4)
+        filter_floor(3)
+        filter_scale(3)
 
-        def is_group(q):
-            return 0 <= q < GROUPS
-
-        last_block_stage = 5
-        first_product_step = HEADS - 1 + last_block_stage
-        last_group_stage = 3
-        for step in range(first_product_step + GROUPS + last_group_stage):
-            summed, scaled, moved, coded = step, step - 3, step - 4, step - last_block_stage
-            pair = (step - 2) // 2 if step % 2 == 0 and 0 < step <= BLOCKS else None
-            made = step - first_product_step
-            squared, added, stored = made - 1, made - 2, made - last_group_stage
-
-            if pair is not None:
-                filter_inverse_length(pair)
-            if is_group(added):
+        x_steps = {0: ((), (2, 3)), 1: ((4, 5), (4, 5)), 2: ((6, 7), (6, 7))}
+        for q in range(GROUPS + 3):
+            squared, added, stored = q - 1, q - 2, q - 3
+            coded, moved, scaled, summed = q + 4, q + 5, q + 6, q + 8
+            pair = summed // 2 if summed % 2 == 1 and summed < BLOCKS else None
+            if FIRST_VECTOR_FOLD <= added < GROUPS:
                 fold_heads(added)
-            if is_group(stored):
-                for h in range(BANKS_PER_GROUP):
-                    scale_and_store(stored, h)
+            if 0 <= stored < GROUPS:
+                scale_products(stored)
+            if 0 <= squared < GROUPS:
+                square_products(squared)
+            if 0 <= added < GROUPS:
+                add_folded_heads(added)
+            if moved < BLOCKS:
+                transpose_filters(moved)
+            regrouped, quantised = x_steps.get(q, ((), ()))
+            for unit in regrouped:
+                regroup_x(unit)
+            for unit in quantised:
+                quantise_x(unit)
+            if 0 <= squared < min(GROUPS, FIRST_VECTOR_FOLD):
+                fold_heads(squared)
+            if summed < BLOCKS:
+                filter_sum_squares(summed)
+                if pair is not None:
+                    filter_inverse_length(pair)
+            if moved < BLOCKS:
+                regroup_filters(moved)
+            if 0 <= added < GROUPS:
+                inverse_rms(added)
             if pair is not None:
                 filter_length(pair)
-            if is_block(coded):
+            if coded < BLOCKS:
                 quantise_filters(coded)
             if pair is not None:
                 filter_floor(pair)
-            if is_block(moved):
-                transpose_filters(moved)
-            if is_group(added):
-                add_folded_heads(added)
-            if is_block(summed):
-                filter_sum_squares(summed)
-            if is_group(squared):
-                square_products(squared)
-            if is_group(added):
-                inverse_rms(added)
-            if is_block(moved):
-                regroup_filters(moved)
-            if is_block(scaled):
+            if scaled < BLOCKS:
                 normalise_filters(scaled)
             if pair is not None:
                 filter_scale(pair)
-            if is_group(made):
-                project(made)
-            unit, quantise = divmod(step - 2, 2)
-            if 0 <= unit < X_UNITS:
-                if quantise:
-                    quantise_x(unit)
-                else:
-                    regroup_x(unit)
+            if 0 < q < GROUPS:
+                project(q)

@@ -55,6 +55,7 @@ def tile_cosineattention_pa_kernel(tc, x, w_attn, out_0, out_1, out_2):
         psum = ctx.enter_context(tc.psum_pool(name="psum", bufs=2))
 
         identity = keep.tile([P, P], F32)
+        deal = keep.tile([P, 2, HALF], F32)
         zero_column = keep.tile([P, 1], F32)
         eps_column = keep.tile([P, 1], F32)
         table_warmer = keep.tile([P, 1], F32)
@@ -95,7 +96,7 @@ def tile_cosineattention_pa_kernel(tc, x, w_attn, out_0, out_1, out_2):
             blocks = slice(BLOCKS_PER_PHASE * phase + first, BLOCKS_PER_PHASE * phase + last)
             for i in range(2):
                 nc.sync.dma_start(
-                    out=w_raw[HALF * i : HALF * (i + 1), blocks, :], in_=w_halves[third, half, i, :, first:last, :]
+                    out=w_raw[i:P:2, blocks, :], in_=w_halves[third, half, i, :, first:last, :]
                 )
 
         def load_everything():
@@ -108,7 +109,8 @@ def tile_cosineattention_pa_kernel(tc, x, w_attn, out_0, out_1, out_2):
             for g in range(PASSES):
                 load_x(g, False)
             for phase in range(2, PHASES):
-                load_filters(phase, 0, BLOCKS_PER_PHASE)
+                load_filters(phase, 0, 2)
+                load_filters(phase, 2, 4)
 
         def regroup_x(unit):
             k, g = divmod(unit, PASSES)
@@ -184,7 +186,7 @@ def tile_cosineattention_pa_kernel(tc, x, w_attn, out_0, out_1, out_2):
             for c in range(PASSES * 2):
                 g, u = divmod(c, 2)
                 start = P * (PASSES * u + g)
-                nc.tensor.transpose(bank[:, c, :], words[:, start : start + P], identity[:])
+                nc.tensor.transpose(bank[:, c, :], words[:, start : start + P], deal[:].rearrange("p i d -> p (i d)"))
             turned[b] = bank
 
         def regroup_filters(b):
@@ -297,6 +299,7 @@ def tile_cosineattention_pa_kernel(tc, x, w_attn, out_0, out_1, out_2):
         nc.vector.tensor_scalar_add(out=tiny_column[:], in0=zero_column[:], scalar1=1e-30)
         nc.scalar.activation(out=table_warmer[:], in_=eps_column[:], func=ACT.Abs_reciprocal_sqrt)
         masks.make_identity(nc, identity[:])
+        nc.vector.tensor_copy(out=deal[:], in_=identity[:].rearrange("p (d i) -> p i d", i=2))
 
         pairs_ahead = BLOCKS_PER_PHASE // 2
         for pair in range(pairs_ahead + 1):

@@ -33,8 +33,6 @@ GROUP_POSITIONS = BANKS_PER_GROUP * P
 GROUPS_PER_PHASE = POSITIONS // GROUP_POSITIONS
 GROUPS = PHASES * GROUPS_PER_PHASE
 X_UNITS = PASSES * GROUPS_PER_PHASE
-FIRST_VECTOR_FOLD = 20
-
 FLOPS = 2 * POSITIONS * CHANNELS * THIRDS * HEADS * HEAD_DIM
 
 
@@ -64,10 +62,10 @@ def tile_cosineattention_pa_kernel(tc, x, w_attn, out_0, out_1, out_2):
         x_late = keep.tile([P, PASSES * PACK, POSITIONS - GROUP_POSITIONS], BF16)
         x_codes = keep.tile([P, PASSES, POSITIONS], U32, align_bytes=64)
         x_scales = keep.tile([P, PASSES, POSITIONS], U8, align_bytes=64)
-        w_raw = keep.tile([P, BLOCKS, CHANNELS], BF16)
         w_codes = keep.tile([P, PHASES, PASSES, BANK], U32, align_bytes=64)
         w_scales = keep.tile([P, PHASES, PASSES, BANK], U8, align_bytes=64)
 
+        w_raw = {}
         sum_squares = {}
         inverse_lengths = {}
         lengths = {}
@@ -79,8 +77,8 @@ def tile_cosineattention_pa_kernel(tc, x, w_attn, out_0, out_1, out_2):
         grouped_x = {}
         products = {}
         squares = {}
-        folded_squares = {}
         head_sums = {}
+        turned_inv_rms = {}
         inv_rms = {}
         finished = {}
 
@@ -93,11 +91,11 @@ def tile_cosineattention_pa_kernel(tc, x, w_attn, out_0, out_1, out_2):
 
         def load_filters(phase, first, last):
             third, half = divmod(phase, 2)
-            blocks = slice(BLOCKS_PER_PHASE * phase + first, BLOCKS_PER_PHASE * phase + last)
+            raw = keep.tile([P, last - first, CHANNELS], BF16, name="w_%d_%d" % (phase, first))
             for i in range(2):
-                nc.sync.dma_start(
-                    out=w_raw[i:P:2, blocks, :], in_=w_halves[third, half, i, :, first:last, :]
-                )
+                nc.sync.dma_start(out=raw[i:P:2], in_=w_halves[third, half, i, :, first:last, :])
+            for j in range(first, last):
+                w_raw[BLOCKS_PER_PHASE * phase + j] = raw[:, j - first, :]
 
         def load_everything():
             for j in range(BLOCKS_PER_PHASE):
@@ -140,7 +138,7 @@ def tile_cosineattention_pa_kernel(tc, x, w_attn, out_0, out_1, out_2):
                 sum_squares[pair] = tiny.tile([P, 2], F32, name="totals")
             unread = w_stage.tile([P, CHANNELS], BF16)
             nc.scalar.activation(
-                out=unread[:], in_=w_raw[:, b, :], func=ACT.Square, accum_out=sum_squares[pair][:, member : member + 1]
+                out=unread[:], in_=w_raw[b], func=ACT.Square, accum_out=sum_squares[pair][:, member : member + 1]
             )
 
         def filter_inverse_length(pair):
@@ -172,7 +170,7 @@ def tile_cosineattention_pa_kernel(tc, x, w_attn, out_0, out_1, out_2):
             wn = w_stage.tile([P, 2, CHANNELS // PACK, 2], BF16)
             nc.vector.tensor_scalar_mul(
                 out=wn[:],
-                in0=w_raw[:, b, :].rearrange("o (r u e) -> o u r e", u=2, e=2),
+                in0=w_raw[b].rearrange("o (r u e) -> o u r e", u=2, e=2),
                 scalar1=filter_scales[pair][:, member : member + 1],
             )
             normed[b] = wn
@@ -211,63 +209,58 @@ def tile_cosineattention_pa_kernel(tc, x, w_attn, out_0, out_1, out_2):
                     in_=grouped_w[b][:, g].rearrange("p o t -> p (o t)"),
                 )
 
-        def project(q):
+        def project(q, j):
             phase, k = divmod(q, GROUPS_PER_PHASE)
-            banks = []
-            for j in range(BANKS_PER_GROUP):
-                columns = slice(GROUP_POSITIONS * k + P * j, GROUP_POSITIONS * k + P * (j + 1))
-                bank = psum.tile([P, HEADS, HALF], F32, tag="product", bufs=6)
-                for g in range(PASSES):
-                    nc.tensor.matmul_mx(
-                        out=bank[:].rearrange("p n d -> p (n d)"),
-                        lhsT=x_codes[:, g, columns].bitcast(FP8X4),
-                        lhsT_scale=x_scales[:, g, columns],
-                        rhs=w_codes[:, phase, g, :].bitcast(FP8X4),
-                        rhs_scale=w_scales[:, phase, g, :],
-                        start=(g == 0),
-                        stop=(g == PASSES - 1),
-                    )
-                banks.append(bank)
-            products[q] = banks
+            columns = slice(GROUP_POSITIONS * k + P * j, GROUP_POSITIONS * k + P * (j + 1))
+            bank = psum.tile([P, HEADS, HALF], F32, tag="product", bufs=6)
+            for g in range(PASSES):
+                nc.tensor.matmul_mx(
+                    out=bank[:].rearrange("p n d -> p (n d)"),
+                    lhsT=x_codes[:, g, columns].bitcast(FP8X4),
+                    lhsT_scale=x_scales[:, g, columns],
+                    rhs=w_codes[:, phase, g, :].bitcast(FP8X4),
+                    rhs_scale=w_scales[:, phase, g, :],
+                    start=(g == 0),
+                    stop=(g == PASSES - 1),
+                )
+            products[q, j] = bank
 
         def square_products(q):
-            sq = norm.tile([P, BANKS_PER_GROUP, HEADS, HALF], F32)
+            sq = norm.tile([P, HEADS, BANKS_PER_GROUP, HALF], F32)
             for j in range(BANKS_PER_GROUP):
-                nc.scalar.activation(out=sq[:, j], in_=products[q][j][:], func=ACT.Square)
+                nc.scalar.activation(out=sq[:, :, j, :], in_=products[q, j][:], func=ACT.Square)
             squares[q] = sq
 
-        def fold_heads(q):
-            folded = norm.tile([P, HEADS // 2, BANKS_PER_GROUP, HALF], F32)
-            engine = nc.gpsimd if q < FIRST_VECTOR_FOLD else nc.vector
-            engine.tensor_tensor(
-                out=folded[:].rearrange("p n j d -> p j n d"),
-                in0=squares[q][:, :, : HEADS // 2, :],
-                in1=squares[q][:, :, HEADS // 2 :, :],
-                op=ALU.add,
-            )
-            folded_squares[q] = folded
-
-        def add_folded_heads(q):
-            total = psum.tile([P, BANKS_PER_GROUP * HALF], F32, tag="head_sum", bufs=1)
-            for n in range(HEADS // 2):
+        def add_heads(q):
+            total = psum.tile([P, 2, P], F32, tag="head_sum", bufs=1)
+            for n in range(HEADS):
                 nc.tensor.matmul(
-                    out=total[:],
-                    lhsT=identity[:],
-                    rhs=folded_squares[q][:, n].rearrange("p j d -> p (j d)"),
+                    out=total[:, 0, :],
+                    lhsT=squares[q][:, n].rearrange("p j d -> p (j d)"),
+                    rhs=identity[:],
+                    is_transpose=True,
                     start=(n == 0),
-                    stop=(n == HEADS // 2 - 1),
+                    stop=(n == HEADS - 1),
                 )
             head_sums[q] = total
 
         def inverse_rms(q):
-            r = norm.tile([P, BANKS_PER_GROUP, HALF], F32)
+            r = norm.tile([P, P], F32, name="turned_rms")
             nc.scalar.activation(
-                out=r[:].rearrange("p j d -> p (j d)"),
-                in_=head_sums[q][:],
+                out=r[:],
+                in_=head_sums[q][:, 0, :],
                 func=ACT.Abs_reciprocal_sqrt,
                 scale=1.0 / HEADS,
                 bias=eps_column[:],
             )
+            turned_inv_rms[q] = r
+
+        def turn_inverse_rms(q):
+            nc.tensor.transpose(head_sums[q][:, 1, :], turned_inv_rms[q][:], identity[:])
+
+        def copy_inverse_rms(q):
+            r = norm.tile([P, BANKS_PER_GROUP, HALF], F32, name="rms")
+            nc.vector.tensor_copy(out=r[:].rearrange("p j d -> p (j d)"), in_=head_sums[q][:, 1, :])
             inv_rms[q] = r
 
         def scale_products(q):
@@ -279,7 +272,7 @@ def tile_cosineattention_pa_kernel(tc, x, w_attn, out_0, out_1, out_2):
             for j in range(BANKS_PER_GROUP):
                 nc.vector.tensor_tensor(
                     out=res[:, :, j, HALF * half : HALF * (half + 1)],
-                    in0=products[q][j][:],
+                    in0=products[q, j][:],
                     in1=inv_rms[q][:, j].unsqueeze(1).to_broadcast([P, HEADS, HALF]),
                     op=ALU.mult,
                 )
@@ -339,7 +332,8 @@ def tile_cosineattention_pa_kernel(tc, x, w_attn, out_0, out_1, out_2):
         filter_sum_squares(7)
         filter_inverse_length(3)
         quantise_filters(3)
-        project(0)
+        project(0, 0)
+        project(0, 1)
         transpose_filters(4)
         regroup_x(2)
         regroup_x(3)
@@ -353,40 +347,40 @@ def tile_cosineattention_pa_kernel(tc, x, w_attn, out_0, out_1, out_2):
             squared, added, stored = q - 1, q - 2, q - 3
             coded, moved, scaled, summed = q + 4, q + 5, q + 6, q + 8
             pair = summed // 2 if summed % 2 == 1 and summed < BLOCKS else None
-            if FIRST_VECTOR_FOLD <= added < GROUPS:
-                fold_heads(added)
             if 0 <= stored < GROUPS:
                 scale_products(stored)
-            if 0 <= squared < GROUPS:
-                square_products(squared)
             if 0 <= added < GROUPS:
-                add_folded_heads(added)
-            if moved < BLOCKS:
-                transpose_filters(moved)
+                add_heads(added)
+            if summed < BLOCKS:
+                filter_sum_squares(summed)
+            if pair is not None:
+                filter_inverse_length(pair)
+                filter_length(pair)
             regrouped, quantised = x_steps.get(q, ((), ()))
             for unit in regrouped:
                 regroup_x(unit)
             for unit in quantised:
                 quantise_x(unit)
-            if 0 <= squared < min(GROUPS, FIRST_VECTOR_FOLD):
-                fold_heads(squared)
-            if summed < BLOCKS:
-                filter_sum_squares(summed)
-                if pair is not None:
-                    filter_inverse_length(pair)
             if moved < BLOCKS:
-                regroup_filters(moved)
+                transpose_filters(moved)
+            if 0 <= squared < GROUPS:
+                square_products(squared)
+            if 0 < q < GROUPS:
+                project(q, 0)
             if 0 <= added < GROUPS:
                 inverse_rms(added)
-            if pair is not None:
-                filter_length(pair)
-            if coded < BLOCKS:
-                quantise_filters(coded)
+            if moved < BLOCKS:
+                regroup_filters(moved)
             if pair is not None:
                 filter_floor(pair)
+            if 0 <= added < GROUPS:
+                turn_inverse_rms(added)
+                copy_inverse_rms(added)
+            if coded < BLOCKS:
+                quantise_filters(coded)
+            if 0 < q < GROUPS:
+                project(q, 1)
             if scaled < BLOCKS:
                 normalise_filters(scaled)
             if pair is not None:
                 filter_scale(pair)
-            if 0 < q < GROUPS:
-                project(q)

@@ -112,15 +112,13 @@ def tile_cosineattention_pa_kernel(tc, x, w_attn, out_0, out_1, out_2):
 
         def regroup_x(unit):
             k, g = divmod(unit, PASSES)
-            grouped = x_stage.tile([P, BANKS_PER_GROUP, P, PACK], BF16, align_bytes=64)
+            grouped = x_stage.tile([P, GROUP_POSITIONS, PACK], BF16, align_bytes=64)
             channels = slice(PACK * g, PACK * (g + 1))
             if k == 0:
                 rows = x_early[:, channels, :]
             else:
                 rows = x_late[:, channels, GROUP_POSITIONS * (k - 1) : GROUP_POSITIONS * k]
-            nc.vector.tensor_copy(
-                out=grouped[:], in_=rows.rearrange("p t (s j) -> p j s t", j=BANKS_PER_GROUP)
-            )
+            nc.vector.tensor_copy(out=grouped[:], in_=rows.rearrange("p t s -> p s t"))
             grouped_x[unit] = grouped
 
         def quantise_x(unit):
@@ -129,7 +127,7 @@ def tile_cosineattention_pa_kernel(tc, x, w_attn, out_0, out_1, out_2):
             nc.vector.quantize_mx(
                 out=x_codes[:, g, columns].bitcast(FP8X4),
                 scales=x_scales[:, g, columns],
-                in_=grouped_x[unit][:].rearrange("p j s t -> p (j s t)"),
+                in_=grouped_x[unit][:].rearrange("p s t -> p (s t)"),
             )
 
         def filter_sum_squares(b):
@@ -266,25 +264,24 @@ def tile_cosineattention_pa_kernel(tc, x, w_attn, out_0, out_1, out_2):
         def scale_products(q):
             phase, k = divmod(q, GROUPS_PER_PHASE)
             third, half = divmod(phase, 2)
-            if half == 0:
-                finished[third, k] = results.tile([P, HEADS, BANKS_PER_GROUP, HEAD_DIM], F32, name="res")
+            whole_rows = third < THIRDS - 1
+            values = slice(HALF * half, HALF * (half + 1))
+            if not (whole_rows and half == 1):
+                finished[third, k] = results.tile([P, BANKS_PER_GROUP, HEADS, HEAD_DIM], F32, name="res")
             res = finished[third, k]
             for j in range(BANKS_PER_GROUP):
                 nc.vector.tensor_tensor(
-                    out=res[:, :, j, HALF * half : HALF * (half + 1)],
+                    out=res[:, j, :, values],
                     in0=products[q, j][:],
                     in1=inv_rms[q][:, j].unsqueeze(1).to_broadcast([P, HEADS, HALF]),
                     op=ALU.mult,
                 )
-            if half == 1:
-                positions = slice(GROUP_POSITIONS * k, GROUP_POSITIONS * (k + 1))
-                for n in range(0, HEADS, HEADS // 2):
-                    nc.sync.dma_start(
-                        out=outs[third][n : n + HEADS // 2, positions, :].rearrange(
-                            "n (p j) d -> p n (j d)", j=BANKS_PER_GROUP
-                        ),
-                        in_=res[:, n : n + HEADS // 2].rearrange("p n j d -> p n (j d)"),
-                    )
+                first = GROUP_POSITIONS * k + P * j
+                rows = outs[third][:, first : first + P, :].rearrange("n p d -> p n d")
+                if not whole_rows:
+                    nc.sync.dma_start(out=rows[:, :, values], in_=res[:, j, :, values])
+                elif half == 1:
+                    nc.sync.dma_start(out=rows, in_=res[:, j])
 
         load_everything()
         nc.vector.memset(zero_column[:], 0.0)

@@ -78,7 +78,7 @@ def tile_cosineattention_pa_kernel(tc, x, w_attn, out_0, out_1, out_2):
         products = {}
         squares = {}
         head_sums = {}
-        turned_inv_rms = {}
+        folded_squares = {}
         inv_rms = {}
         finished = {}
 
@@ -187,7 +187,7 @@ def tile_cosineattention_pa_kernel(tc, x, w_attn, out_0, out_1, out_2):
 
         def regroup_filters(b):
             grouped = w_stage.tile([P, PASSES, P, PACK], BF16, align_bytes=64)
-            copy = nc.scalar.copy if b == BLOCKS_PER_PHASE - 1 else nc.vector.tensor_copy
+            copy = nc.scalar.copy if b == 2 or (b > 0 and b % 3 == 0) else nc.vector.tensor_copy
             copy(
                 out=grouped[:]
                 .rearrange("p g o t -> p (g o t)")
@@ -223,65 +223,62 @@ def tile_cosineattention_pa_kernel(tc, x, w_attn, out_0, out_1, out_2):
                 )
             products[q, j] = bank
 
-        def square_products(q):
-            sq = norm.tile([P, HEADS, BANKS_PER_GROUP, HALF], F32)
-            for j in range(BANKS_PER_GROUP):
-                nc.scalar.activation(out=sq[:, :, j, :], in_=products[q, j][:], func=ACT.Square)
-            squares[q] = sq
+        def square_products(q, j):
+            if j == 0:
+                squares[q] = norm.tile([P, HEADS, BANKS_PER_GROUP, HALF], F32, name="sq")
+            nc.scalar.activation(out=squares[q][:, :, j, :], in_=products[q, j][:], func=ACT.Square)
 
-        def add_heads(q):
-            total = psum.tile([P, 2, P], F32, tag="head_sum", bufs=1)
-            for n in range(HEADS):
+        def fold_heads(q):
+            four = norm.tile([P, HEADS // 2, P], F32)
+            eight = squares[q][:].rearrange("p n j d -> p n (j d)")
+            nc.vector.tensor_tensor(
+                out=four[:], in0=eight[:, : HEADS // 2], in1=eight[:, HEADS // 2 :], op=ALU.add
+            )
+            folded_squares[q] = four
+
+        def add_folded_heads(q):
+            total = psum.tile([P, P], F32, tag="head_sum", bufs=1)
+            for n in range(HEADS // 2):
                 nc.tensor.matmul(
-                    out=total[:, 0, :],
-                    lhsT=squares[q][:, n].rearrange("p j d -> p (j d)"),
-                    rhs=identity[:],
-                    is_transpose=True,
+                    out=total[:],
+                    lhsT=identity[:],
+                    rhs=folded_squares[q][:, n],
                     start=(n == 0),
-                    stop=(n == HEADS - 1),
+                    stop=(n == HEADS // 2 - 1),
                 )
             head_sums[q] = total
 
         def inverse_rms(q):
-            r = norm.tile([P, P], F32, name="turned_rms")
+            r = norm.tile([P, BANKS_PER_GROUP, HALF], F32)
             nc.scalar.activation(
-                out=r[:],
-                in_=head_sums[q][:, 0, :],
+                out=r[:].rearrange("p j d -> p (j d)"),
+                in_=head_sums[q][:],
                 func=ACT.Abs_reciprocal_sqrt,
                 scale=1.0 / HEADS,
                 bias=eps_column[:],
             )
-            turned_inv_rms[q] = r
-
-        def turn_inverse_rms(q):
-            nc.tensor.transpose(head_sums[q][:, 1, :], turned_inv_rms[q][:], identity[:])
-
-        def copy_inverse_rms(q):
-            r = norm.tile([P, BANKS_PER_GROUP, HALF], F32, name="rms")
-            nc.vector.tensor_copy(out=r[:].rearrange("p j d -> p (j d)"), in_=head_sums[q][:, 1, :])
             inv_rms[q] = r
 
-        def scale_products(q):
+        def scale_products(q, j):
             phase, k = divmod(q, GROUPS_PER_PHASE)
             third, half = divmod(phase, 2)
             whole_rows = third < THIRDS - 1
             values = slice(HALF * half, HALF * (half + 1))
-            if not (whole_rows and half == 1):
+            if j == 0 and not (whole_rows and half == 1):
                 finished[third, k] = results.tile([P, BANKS_PER_GROUP, HEADS, HEAD_DIM], F32, name="res")
             res = finished[third, k]
-            for j in range(BANKS_PER_GROUP):
-                nc.vector.tensor_tensor(
-                    out=res[:, j, :, values],
-                    in0=products[q, j][:],
-                    in1=inv_rms[q][:, j].unsqueeze(1).to_broadcast([P, HEADS, HALF]),
-                    op=ALU.mult,
-                )
-                first = GROUP_POSITIONS * k + P * j
-                rows = outs[third][:, first : first + P, :].rearrange("n p d -> p n d")
-                if not whole_rows:
-                    nc.sync.dma_start(out=rows[:, :, values], in_=res[:, j, :, values])
-                elif half == 1:
-                    nc.sync.dma_start(out=rows, in_=res[:, j])
+            nc.vector.tensor_tensor(
+                out=res[:, j, :, values],
+                in0=products[q, j][:],
+                in1=inv_rms[q][:, j].unsqueeze(1).to_broadcast([P, HEADS, HALF]),
+                op=ALU.mult,
+            )
+            first = GROUP_POSITIONS * k + P * j
+            rows = outs[third][:, first : first + P, :].rearrange("n p d -> p n d")
+            if not whole_rows:
+                nc.sync.dma_start(out=rows[:, :, values], in_=res[:, j, :, values])
+            elif half == 1:
+                nc.sync.dma_start(out=rows, in_=res[:, j])
 
         load_everything()
         nc.vector.memset(zero_column[:], 0.0)
@@ -327,57 +324,58 @@ def tile_cosineattention_pa_kernel(tc, x, w_attn, out_0, out_1, out_2):
                 transpose_filters(b)
         filter_sum_squares(6)
         filter_sum_squares(7)
-        filter_inverse_length(3)
         quantise_filters(3)
         project(0, 0)
         project(0, 1)
         transpose_filters(4)
         regroup_x(2)
         regroup_x(3)
-        filter_length(3)
+        quantise_x(2)
+        quantise_x(3)
         regroup_filters(4)
-        filter_floor(3)
-        filter_scale(3)
 
-        x_steps = {0: ((), (2, 3)), 1: ((4, 5), (4, 5)), 2: ((6, 7), (6, 7))}
+        x_steps = {0: ((4, 5), ()), 1: ((6,), (4, 5)), 2: ((7,), (6, 7))}
         for q in range(GROUPS + 3):
             squared, added, stored = q - 1, q - 2, q - 3
             coded, moved, scaled, summed = q + 4, q + 5, q + 6, q + 8
-            pair = summed // 2 if summed % 2 == 1 and summed < BLOCKS else None
-            if 0 <= stored < GROUPS:
-                scale_products(stored)
+            pair = scaled // 2 if scaled % 2 == 0 and scaled < BLOCKS else None
+            if 0 <= squared < GROUPS:
+                square_products(squared, 0)
             if 0 <= added < GROUPS:
-                add_heads(added)
-            if summed < BLOCKS:
-                filter_sum_squares(summed)
+                add_folded_heads(added)
+            if moved < BLOCKS:
+                transpose_filters(moved)
             if pair is not None:
                 filter_inverse_length(pair)
+            if 0 <= stored < GROUPS:
+                scale_products(stored, 0)
+            if pair is not None:
                 filter_length(pair)
+            if 0 <= squared < GROUPS:
+                square_products(squared, 1)
+            if 0 <= stored < GROUPS:
+                scale_products(stored, 1)
             regrouped, quantised = x_steps.get(q, ((), ()))
             for unit in regrouped:
                 regroup_x(unit)
             for unit in quantised:
                 quantise_x(unit)
-            if moved < BLOCKS:
-                transpose_filters(moved)
-            if 0 <= squared < GROUPS:
-                square_products(squared)
-            if 0 < q < GROUPS:
-                project(q, 0)
+            if pair is not None:
+                filter_floor(pair)
+            if summed < BLOCKS:
+                filter_sum_squares(summed)
             if 0 <= added < GROUPS:
                 inverse_rms(added)
+            if 0 <= squared < GROUPS:
+                fold_heads(squared)
             if moved < BLOCKS:
                 regroup_filters(moved)
             if pair is not None:
-                filter_floor(pair)
-            if 0 <= added < GROUPS:
-                turn_inverse_rms(added)
-                copy_inverse_rms(added)
+                filter_scale(pair)
             if coded < BLOCKS:
                 quantise_filters(coded)
-            if 0 < q < GROUPS:
-                project(q, 1)
             if scaled < BLOCKS:
                 normalise_filters(scaled)
-            if pair is not None:
-                filter_scale(pair)
+            if 0 < q < GROUPS:
+                project(q, 0)
+                project(q, 1)

@@ -112,13 +112,15 @@ def tile_cosineattention_pa_kernel(tc, x, w_attn, out_0, out_1, out_2):
 
         def regroup_x(unit):
             k, g = divmod(unit, PASSES)
-            grouped = x_stage.tile([P, GROUP_POSITIONS, PACK], BF16, align_bytes=64)
+            grouped = x_stage.tile([P, BANKS_PER_GROUP, P, PACK], BF16, align_bytes=64)
             channels = slice(PACK * g, PACK * (g + 1))
             if k == 0:
                 rows = x_early[:, channels, :]
             else:
                 rows = x_late[:, channels, GROUP_POSITIONS * (k - 1) : GROUP_POSITIONS * k]
-            nc.vector.tensor_copy(out=grouped[:], in_=rows.rearrange("p t s -> p s t"))
+            nc.vector.tensor_copy(
+                out=grouped[:], in_=rows.rearrange("p t (s j) -> p j s t", j=BANKS_PER_GROUP)
+            )
             grouped_x[unit] = grouped
 
         def quantise_x(unit):
@@ -127,7 +129,7 @@ def tile_cosineattention_pa_kernel(tc, x, w_attn, out_0, out_1, out_2):
             nc.vector.quantize_mx(
                 out=x_codes[:, g, columns].bitcast(FP8X4),
                 scales=x_scales[:, g, columns],
-                in_=grouped_x[unit][:].rearrange("p s t -> p (s t)"),
+                in_=grouped_x[unit][:].rearrange("p j s t -> p (j s t)"),
             )
 
         def filter_sum_squares(b):
@@ -265,20 +267,25 @@ def tile_cosineattention_pa_kernel(tc, x, w_attn, out_0, out_1, out_2):
             whole_rows = third < THIRDS - 1
             values = slice(HALF * half, HALF * (half + 1))
             if j == 0 and not (whole_rows and half == 1):
-                finished[third, k] = results.tile([P, BANKS_PER_GROUP, HEADS, HEAD_DIM], F32, name="res")
+                finished[third, k] = results.tile([P, HEADS, BANKS_PER_GROUP, HEAD_DIM], F32, name="res")
             res = finished[third, k]
             nc.vector.tensor_tensor(
-                out=res[:, j, :, values],
+                out=res[:, :, j, values],
                 in0=products[q, j][:],
                 in1=inv_rms[q][:, j].unsqueeze(1).to_broadcast([P, HEADS, HALF]),
                 op=ALU.mult,
             )
-            first = GROUP_POSITIONS * k + P * j
-            rows = outs[third][:, first : first + P, :].rearrange("n p d -> p n d")
+            positions = slice(GROUP_POSITIONS * k, GROUP_POSITIONS * (k + 1))
+            rows = outs[third][:, positions, :].rearrange("n (p j) d -> p n j d", j=BANKS_PER_GROUP)
             if not whole_rows:
-                nc.sync.dma_start(out=rows[:, :, values], in_=res[:, j, :, values])
-            elif half == 1:
-                nc.sync.dma_start(out=rows, in_=res[:, j])
+                nc.sync.dma_start(out=rows[:, :, j, values], in_=res[:, :, j, values])
+            elif half == 1 and j == BANKS_PER_GROUP - 1:
+                for n in range(0, HEADS, HEADS // 2):
+                    heads = slice(n, n + HEADS // 2)
+                    nc.sync.dma_start(
+                        out=rows[:, heads].rearrange("p n j d -> p n (j d)"),
+                        in_=res[:, heads].rearrange("p n j d -> p n (j d)"),
+                    )
 
         load_everything()
         nc.vector.memset(zero_column[:], 0.0)

@@ -60,10 +60,10 @@ def tile_cosineattention_pa_kernel(tc, x, w_attn, out_0, out_1, out_2):
         tiny_column = keep.tile([P, 1], F32)
         x_early = keep.tile([P, PASSES * PACK, GROUP_POSITIONS], BF16)
         x_late = keep.tile([P, PASSES * PACK, POSITIONS - GROUP_POSITIONS], BF16)
-        x_codes = keep.tile([P, PASSES, POSITIONS], U32, align_bytes=64)
-        x_scales = keep.tile([P, PASSES, POSITIONS], U8, align_bytes=64)
-        w_codes = keep.tile([P, PHASES, PASSES, BANK], U32, align_bytes=64)
-        w_scales = keep.tile([P, PHASES, PASSES, BANK], U8, align_bytes=64)
+        x_codes = keep.tile([P, PASSES, POSITIONS], U32, align_bytes=256)
+        x_scales = keep.tile([P, PASSES, POSITIONS], U8, align_bytes=256)
+        w_codes = keep.tile([P, PHASES, PASSES, BANK], U32, align_bytes=256)
+        w_scales = keep.tile([P, PHASES, PASSES, BANK], U8, align_bytes=256)
 
         w_raw = {}
         sum_squares = {}

@@ -264,7 +264,7 @@ def tile_cosineattention_pa_kernel(tc, x, w_attn, out_0, out_1, out_2):
         def scale_products(q, j):
             phase, k = divmod(q, GROUPS_PER_PHASE)
             third, half = divmod(phase, 2)
-            whole_rows = third < THIRDS - 1
+            whole_rows = third == 0
             values = slice(HALF * half, HALF * (half + 1))
             if j == 0 and not (whole_rows and half == 1):
                 finished[third, k] = results.tile([P, HEADS, BANKS_PER_GROUP, HEAD_DIM], F32, name="res")

@@ -49,7 +49,7 @@ def tile_cosineattention_pa_kernel(tc, x, w_attn, out_0, out_1, out_2):
         w_stage = ctx.enter_context(tc.tile_pool(name="w_stage", bufs=3))
         tiny = ctx.enter_context(tc.tile_pool(name="tiny", bufs=3))
         norm = ctx.enter_context(tc.tile_pool(name="norm", bufs=3))
-        results = ctx.enter_context(tc.tile_pool(name="results", bufs=6))
+        results = ctx.enter_context(tc.tile_pool(name="results", bufs=12))
         psum = ctx.enter_context(tc.psum_pool(name="psum", bufs=2))
 
         identity = keep.tile([P, P], F32)
@@ -80,7 +80,6 @@ def tile_cosineattention_pa_kernel(tc, x, w_attn, out_0, out_1, out_2):
         head_sums = {}
         folded_squares = {}
         inv_rms = {}
-        finished = {}
 
         def load_x(g, early):
             rows = x_rows[PACK * P * g : PACK * P * (g + 1), :].rearrange("(p t) s -> p t s", t=PACK)
@@ -112,14 +111,15 @@ def tile_cosineattention_pa_kernel(tc, x, w_attn, out_0, out_1, out_2):
 
         def regroup_x(unit):
             k, g = divmod(unit, PASSES)
-            grouped = x_stage.tile([P, BANKS_PER_GROUP, P, PACK], BF16, align_bytes=64)
+            grouped = x_stage.tile([P, GROUP_POSITIONS, PACK], BF16, align_bytes=64)
             channels = slice(PACK * g, PACK * (g + 1))
             if k == 0:
                 rows = x_early[:, channels, :]
             else:
                 rows = x_late[:, channels, GROUP_POSITIONS * (k - 1) : GROUP_POSITIONS * k]
             nc.vector.tensor_copy(
-                out=grouped[:], in_=rows.rearrange("p t (s j) -> p j s t", j=BANKS_PER_GROUP)
+                out=grouped[:].rearrange("p (c i) t -> p c t i", i=4),
+                in_=rows.rearrange("p t (c i) -> p c t i", i=4),
             )
             grouped_x[unit] = grouped
 
@@ -129,7 +129,7 @@ def tile_cosineattention_pa_kernel(tc, x, w_attn, out_0, out_1, out_2):
             nc.vector.quantize_mx(
                 out=x_codes[:, g, columns].bitcast(FP8X4),
                 scales=x_scales[:, g, columns],
-                in_=grouped_x[unit][:].rearrange("p j s t -> p (j s t)"),
+                in_=grouped_x[unit][:].rearrange("p s t -> p (s t)"),
             )
 
         def filter_sum_squares(b):
@@ -264,28 +264,17 @@ def tile_cosineattention_pa_kernel(tc, x, w_attn, out_0, out_1, out_2):
         def scale_products(q, j):
             phase, k = divmod(q, GROUPS_PER_PHASE)
             third, half = divmod(phase, 2)
-            whole_rows = third == 0
             values = slice(HALF * half, HALF * (half + 1))
-            if j == 0 and not (whole_rows and half == 1):
-                finished[third, k] = results.tile([P, HEADS, BANKS_PER_GROUP, HEAD_DIM], F32, name="res")
-            res = finished[third, k]
+            res = results.tile([P, HEADS, HALF], F32)
             nc.vector.tensor_tensor(
-                out=res[:, :, j, values],
+                out=res[:],
                 in0=products[q, j][:],
                 in1=inv_rms[q][:, j].unsqueeze(1).to_broadcast([P, HEADS, HALF]),
                 op=ALU.mult,
             )
-            positions = slice(GROUP_POSITIONS * k, GROUP_POSITIONS * (k + 1))
-            rows = outs[third][:, positions, :].rearrange("n (p j) d -> p n j d", j=BANKS_PER_GROUP)
-            if not whole_rows:
-                nc.sync.dma_start(out=rows[:, :, j, values], in_=res[:, :, j, values])
-            elif half == 1 and j == BANKS_PER_GROUP - 1:
-                for n in range(0, HEADS, HEADS // 2):
-                    heads = slice(n, n + HEADS // 2)
-                    nc.sync.dma_start(
-                        out=rows[:, heads].rearrange("p n j d -> p n (j d)"),
-                        in_=res[:, heads].rearrange("p n j d -> p n (j d)"),
-                    )
+            start = GROUP_POSITIONS * k + P * j
+            rows = outs[third][:, start : start + P, values].rearrange("n p d -> p n d")
+            nc.sync.dma_start(out=rows, in_=res[:])
 
         load_everything()
         nc.vector.memset(zero_column[:], 0.0)

@@ -58,17 +58,16 @@ def tile_cosineattention_pa_kernel(tc, x, w_attn, out_0, out_1, out_2):
         eps_column = keep.tile([P, 1], F32)
         table_warmer = keep.tile([P, 1], F32)
         tiny_column = keep.tile([P, 1], F32)
-        x_early = keep.tile([P, PASSES * PACK, GROUP_POSITIONS], BF16)
-        x_late = keep.tile([P, PASSES * PACK, POSITIONS - GROUP_POSITIONS], BF16)
+        one_column = keep.tile([P, 1], F32)
         x_codes = keep.tile([P, PASSES, POSITIONS], U32, align_bytes=256)
         x_scales = keep.tile([P, PASSES, POSITIONS], U8, align_bytes=256)
         w_codes = keep.tile([P, PHASES, PASSES, BANK], U32, align_bytes=256)
         w_scales = keep.tile([P, PHASES, PASSES, BANK], U8, align_bytes=256)
 
+        x_raw = {}
         w_raw = {}
         sum_squares = {}
         inverse_lengths = {}
-        lengths = {}
         padded_lengths = {}
         filter_scales = {}
         normed = {}
@@ -81,12 +80,12 @@ def tile_cosineattention_pa_kernel(tc, x, w_attn, out_0, out_1, out_2):
         folded_squares = {}
         inv_rms = {}
 
-        def load_x(g, early):
+        def load_x(g, first, last):
             rows = x_rows[PACK * P * g : PACK * P * (g + 1), :].rearrange("(p t) s -> p t s", t=PACK)
-            nc.sync.dma_start(
-                out=(x_early if early else x_late)[:, PACK * g : PACK * (g + 1), :],
-                in_=rows[:, :, :GROUP_POSITIONS] if early else rows[:, :, GROUP_POSITIONS:],
-            )
+            raw = keep.tile([P, PACK, GROUP_POSITIONS * (last - first)], BF16, name="x_%d_%d" % (g, first))
+            nc.sync.dma_start(out=raw[:], in_=rows[:, :, GROUP_POSITIONS * first : GROUP_POSITIONS * last])
+            for k in range(first, last):
+                x_raw[k, g] = raw[:, :, GROUP_POSITIONS * (k - first) : GROUP_POSITIONS * (k - first + 1)]
 
         def load_filters(phase, first, last):
             third, half = divmod(phase, 2)
@@ -99,12 +98,15 @@ def tile_cosineattention_pa_kernel(tc, x, w_attn, out_0, out_1, out_2):
         def load_everything():
             for j in range(BLOCKS_PER_PHASE):
                 load_filters(0, j, j + 1)
-                if j < PASSES:
-                    load_x(j, True)
-            load_filters(1, 0, 2)
+            for g in range(PASSES):
+                load_x(g, 0, 1)
+            load_filters(1, 0, 1)
+            load_filters(1, 1, 2)
+            for g in range(PASSES):
+                load_x(g, 1, 2)
             load_filters(1, 2, 4)
             for g in range(PASSES):
-                load_x(g, False)
+                load_x(g, 2, 4)
             for phase in range(2, PHASES):
                 load_filters(phase, 0, 2)
                 load_filters(phase, 2, 4)
@@ -112,11 +114,7 @@ def tile_cosineattention_pa_kernel(tc, x, w_attn, out_0, out_1, out_2):
         def regroup_x(unit):
             k, g = divmod(unit, PASSES)
             grouped = x_stage.tile([P, GROUP_POSITIONS, PACK], BF16, align_bytes=64)
-            channels = slice(PACK * g, PACK * (g + 1))
-            if k == 0:
-                rows = x_early[:, channels, :]
-            else:
-                rows = x_late[:, channels, GROUP_POSITIONS * (k - 1) : GROUP_POSITIONS * k]
+            rows = x_raw[k, g]
             nc.vector.tensor_copy(
                 out=grouped[:].rearrange("p (c i) t -> p c t i", i=4),
                 in_=rows.rearrange("p t (c i) -> p c t i", i=4),
@@ -137,9 +135,13 @@ def tile_cosineattention_pa_kernel(tc, x, w_attn, out_0, out_1, out_2):
             if member == 0:
                 sum_squares[pair] = tiny.tile([P, 2], F32, name="totals")
             unread = w_stage.tile([P, CHANNELS], BF16)
-            nc.scalar.activation(
-                out=unread[:], in_=w_raw[b], func=ACT.Square, accum_out=sum_squares[pair][:, member : member + 1]
-            )
+            total = sum_squares[pair][:, member : member + 1]
+            if b == 1:
+                nc.vector.scalar_tensor_tensor(
+                    out=unread[:], in0=w_raw[b], scalar=1.0, in1=w_raw[b], op0=ALU.mult, op1=ALU.mult, accum_out=total
+                )
+            else:
+                nc.scalar.activation(out=unread[:], in_=w_raw[b], func=ACT.Square, accum_out=total)
 
         def filter_inverse_length(pair):
             inverse = tiny.tile([P, 2], F32)
@@ -148,16 +150,11 @@ def tile_cosineattention_pa_kernel(tc, x, w_attn, out_0, out_1, out_2):
             )
             inverse_lengths[pair] = inverse
 
-        def filter_length(pair):
-            length = tiny.tile([P, 2], F32)
-            nc.vector.tensor_tensor(
-                out=length[:], in0=sum_squares[pair][:], in1=inverse_lengths[pair][:], op=ALU.mult
-            )
-            lengths[pair] = length
-
         def filter_floor(pair):
             padded = tiny.tile([P, 2], F32)
-            nc.vector.tensor_scalar_add(out=padded[:], in0=lengths[pair][:], scalar1=NORM_FLOOR)
+            nc.scalar.activation(
+                out=padded[:], in_=inverse_lengths[pair][:], func=ACT.Identity, scale=NORM_FLOOR, bias=one_column[:]
+            )
             padded_lengths[pair] = padded
 
         def filter_scale(pair):
@@ -168,10 +165,13 @@ def tile_cosineattention_pa_kernel(tc, x, w_attn, out_0, out_1, out_2):
         def normalise_filters(b):
             pair, member = divmod(b, 2)
             wn = w_stage.tile([P, 2, CHANNELS // PACK, 2], BF16)
-            nc.vector.tensor_scalar_mul(
+            nc.vector.tensor_scalar(
                 out=wn[:],
                 in0=w_raw[b].rearrange("o (r u e) -> o u r e", u=2, e=2),
-                scalar1=filter_scales[pair][:, member : member + 1],
+                scalar1=inverse_lengths[pair][:, member : member + 1],
+                scalar2=filter_scales[pair][:, member : member + 1],
+                op0=ALU.mult,
+                op1=ALU.mult,
             )
             normed[b] = wn
 
@@ -189,7 +189,8 @@ def tile_cosineattention_pa_kernel(tc, x, w_attn, out_0, out_1, out_2):
 
         def regroup_filters(b):
             grouped = w_stage.tile([P, PASSES, P, PACK], BF16, align_bytes=64)
-            copy = nc.scalar.copy if b == 2 or (b > 0 and b % 3 == 0) else nc.vector.tensor_copy
+            on_scalar = b < 3 if b < BLOCKS_PER_PHASE else b % 2 == 1
+            copy = nc.scalar.copy if on_scalar else nc.vector.tensor_copy
             copy(
                 out=grouped[:]
                 .rearrange("p g o t -> p (g o t)")
@@ -279,99 +280,98 @@ def tile_cosineattention_pa_kernel(tc, x, w_attn, out_0, out_1, out_2):
         load_everything()
         nc.vector.memset(zero_column[:], 0.0)
         nc.vector.tensor_scalar_add(out=eps_column[:], in0=zero_column[:], scalar1=EPS)
+        nc.vector.memset(one_column[:], 1.0)
         nc.vector.tensor_scalar_add(out=tiny_column[:], in0=zero_column[:], scalar1=1e-30)
         nc.scalar.activation(out=table_warmer[:], in_=eps_column[:], func=ACT.Abs_reciprocal_sqrt)
         masks.make_identity(nc, identity[:])
         nc.vector.tensor_copy(out=deal[:], in_=identity[:].rearrange("p (d i) -> p i d", i=2))
 
-        pairs_ahead = BLOCKS_PER_PHASE // 2
-        for pair in range(pairs_ahead + 1):
-            a, b = 2 * pair, 2 * pair + 1
-            turning = pair < pairs_ahead
-            filter_sum_squares(a)
+        for b in range(3):
             filter_sum_squares(b)
-            filter_inverse_length(pair)
-            if pair == 0:
-                regroup_x(0)
-                regroup_x(1)
-                filter_length(pair)
-                quantise_x(0)
-                filter_floor(pair)
-                quantise_x(1)
-                filter_scale(pair)
-                normalise_filters(a)
-                transpose_filters(a)
-                normalise_filters(b)
-                transpose_filters(b)
-                continue
-            filter_length(pair)
-            regroup_filters(a - 2)
-            filter_floor(pair)
-            if pair > 1:
-                quantise_filters(a - 3)
-            filter_scale(pair)
-            regroup_filters(a - 1)
-            normalise_filters(a)
-            if turning:
-                transpose_filters(a)
-            quantise_filters(a - 2)
+        filter_inverse_length(0)
+        filter_sum_squares(3)
+        filter_floor(0)
+        filter_scale(0)
+        regroup_x(0)
+        for b in range(2):
             normalise_filters(b)
-            if turning:
-                transpose_filters(b)
-        filter_sum_squares(6)
-        filter_sum_squares(7)
+            transpose_filters(b)
+        filter_inverse_length(1)
+        filter_floor(1)
+        filter_scale(1)
+        regroup_x(1)
+        filter_sum_squares(4)
+        for b in range(2, 4):
+            normalise_filters(b)
+            transpose_filters(b)
+        regroup_filters(0)
+        regroup_filters(1)
+        quantise_x(0)
+        quantise_x(1)
+        regroup_filters(2)
+        quantise_filters(0)
+        regroup_filters(3)
+        quantise_filters(1)
+        quantise_filters(2)
         quantise_filters(3)
-        project(0, 0)
-        project(0, 1)
-        transpose_filters(4)
+        filter_sum_squares(5)
         regroup_x(2)
         regroup_x(3)
+        filter_inverse_length(2)
+        filter_floor(2)
+        filter_scale(2)
         quantise_x(2)
         quantise_x(3)
-        regroup_filters(4)
+        filter_sum_squares(6)
 
-        x_steps = {0: ((4, 5), ()), 1: ((6,), (4, 5)), 2: ((7,), (6, 7))}
         for q in range(GROUPS + 3):
             squared, added, stored = q - 1, q - 2, q - 3
-            coded, moved, scaled, summed = q + 4, q + 5, q + 6, q + 8
-            pair = scaled // 2 if scaled % 2 == 0 and scaled < BLOCKS else None
+            coded, moved, summed = q + 3, q + 4, q + 7
+            pair = (q + 5) // 2 if q % 2 == 1 and q + 5 < BLOCKS else None
             if 0 <= squared < GROUPS:
                 square_products(squared, 0)
-            if 0 <= added < GROUPS:
-                add_folded_heads(added)
-            if moved < BLOCKS:
-                transpose_filters(moved)
             if pair is not None:
                 filter_inverse_length(pair)
-            if 0 <= stored < GROUPS:
-                scale_products(stored, 0)
-            if pair is not None:
-                filter_length(pair)
             if 0 <= squared < GROUPS:
                 square_products(squared, 1)
-            if 0 <= stored < GROUPS:
-                scale_products(stored, 1)
-            regrouped, quantised = x_steps.get(q, ((), ()))
-            for unit in regrouped:
-                regroup_x(unit)
-            for unit in quantised:
-                quantise_x(unit)
             if pair is not None:
                 filter_floor(pair)
+            if 0 <= added < GROUPS:
+                add_folded_heads(added)
+            if q == 2:
+                regroup_x(6)
+                regroup_x(7)
+            if q < 2:
+                project(q, 0)
+                project(q, 1)
+            if moved < BLOCKS:
+                normalise_filters(moved)
+                transpose_filters(moved)
+            if 0 <= stored < GROUPS:
+                scale_products(stored, 0)
+            if q > 0 and coded < BLOCKS:
+                quantise_filters(coded)
+            if 0 <= stored < GROUPS:
+                scale_products(stored, 1)
             if summed < BLOCKS:
                 filter_sum_squares(summed)
             if 0 <= added < GROUPS:
                 inverse_rms(added)
             if 0 <= squared < GROUPS:
                 fold_heads(squared)
-            if moved < BLOCKS:
-                regroup_filters(moved)
+            if q == 0:
+                regroup_x(4)
+                regroup_x(5)
+            if q == 2:
+                quantise_x(6)
+                quantise_x(7)
             if pair is not None:
                 filter_scale(pair)
-            if coded < BLOCKS:
-                quantise_filters(coded)
-            if scaled < BLOCKS:
-                normalise_filters(scaled)
-            if 0 < q < GROUPS:
+            if moved < BLOCKS:
+                regroup_filters(moved)
+            if q == 0:
+                quantise_x(4)
+                quantise_x(5)
+            if 2 <= q < GROUPS:
                 project(q, 0)
                 project(q, 1)

@@ -189,7 +189,7 @@ def tile_cosineattention_pa_kernel(tc, x, w_attn, out_0, out_1, out_2):
 
         def regroup_filters(b):
             grouped = w_stage.tile([P, PASSES, P, PACK], BF16, align_bytes=64)
-            on_scalar = b < 3 if b < BLOCKS_PER_PHASE else b % 2 == 1
+            on_scalar = b < 3 if b < BLOCKS_PER_PHASE else b % 3 == 2
             copy = nc.scalar.copy if on_scalar else nc.vector.tensor_copy
             copy(
                 out=grouped[:]

@@ -239,15 +239,27 @@ def tile_cosineattention_pa_kernel(tc, x, w_attn, out_0, out_1, out_2):
             )
             folded_squares[q] = four
 
+        def fold_twice(q):
+            two = norm.tile([P, HEADS // 4, P], F32)
+            four = folded_squares[q]
+            nc.vector.tensor_tensor(
+                out=two[:], in0=four[:, : HEADS // 4], in1=four[:, HEADS // 4 :], op=ALU.add
+            )
+            folded_squares[q] = two
+
+        def folded_twice(q):
+            return q >= 17 and q % 2 == 1
+
         def add_folded_heads(q):
             total = psum.tile([P, P], F32, tag="head_sum", bufs=1)
-            for n in range(HEADS // 2):
+            left = HEADS // 4 if folded_twice(q) else HEADS // 2
+            for n in range(left):
                 nc.tensor.matmul(
                     out=total[:],
                     lhsT=identity[:],
                     rhs=folded_squares[q][:, n],
                     start=(n == 0),
-                    stop=(n == HEADS // 2 - 1),
+                    stop=(n == left - 1),
                 )
             head_sums[q] = total
 
@@ -372,6 +384,8 @@ def tile_cosineattention_pa_kernel(tc, x, w_attn, out_0, out_1, out_2):
             if q == 0:
                 quantise_x(4)
                 quantise_x(5)
+            if 0 <= squared < GROUPS and folded_twice(squared):
+                fold_twice(squared)
             if 2 <= q < GROUPS:
                 project(q, 0)
                 project(q, 1)

@@ -189,7 +189,7 @@ def tile_cosineattention_pa_kernel(tc, x, w_attn, out_0, out_1, out_2):
 
         def regroup_filters(b):
             grouped = w_stage.tile([P, PASSES, P, PACK], BF16, align_bytes=64)
-            on_scalar = b < 3 if b < BLOCKS_PER_PHASE else b % 3 == 2
+            on_scalar = b < 3 if b < BLOCKS_PER_PHASE else b % 3 == 2 or b >= 20
             copy = nc.scalar.copy if on_scalar else nc.vector.tensor_copy
             copy(
                 out=grouped[:]
@@ -287,7 +287,8 @@ def tile_cosineattention_pa_kernel(tc, x, w_attn, out_0, out_1, out_2):
             )
             start = GROUP_POSITIONS * k + P * j
             rows = outs[third][:, start : start + P, values].rearrange("n p d -> p n d")
-            nc.sync.dma_start(out=rows, in_=res[:])
+            queue = nc.gpsimd if q == GROUPS - GROUPS_PER_PHASE and j == 0 else nc.sync
+            queue.dma_start(out=rows, in_=res[:])
 
         load_everything()
         nc.vector.memset(zero_column[:], 0.0)

@@ -287,7 +287,7 @@ def tile_cosineattention_pa_kernel(tc, x, w_attn, out_0, out_1, out_2):
             )
             start = GROUP_POSITIONS * k + P * j
             rows = outs[third][:, start : start + P, values].rearrange("n p d -> p n d")
-            queue = nc.gpsimd if q == GROUPS - GROUPS_PER_PHASE and j == 0 else nc.sync
+            queue = nc.gpsimd if q == 18 and j == 0 else nc.sync
             queue.dma_start(out=rows, in_=res[:])
 
         load_everything()

@@ -79,6 +79,7 @@ def tile_cosineattention_pa_kernel(tc, x, w_attn, out_0, out_1, out_2):
         head_sums = {}
         folded_squares = {}
         inv_rms = {}
+        finished = {}
 
         def load_x(g, first, last):
             rows = x_rows[PACK * P * g : PACK * P * (g + 1), :].rearrange("(p t) s -> p t s", t=PACK)
@@ -275,9 +276,6 @@ def tile_cosineattention_pa_kernel(tc, x, w_attn, out_0, out_1, out_2):
             inv_rms[q] = r
 
         def scale_products(q, j):
-            phase, k = divmod(q, GROUPS_PER_PHASE)
-            third, half = divmod(phase, 2)
-            values = slice(HALF * half, HALF * (half + 1))
             res = results.tile([P, HEADS, HALF], F32)
             nc.vector.tensor_tensor(
                 out=res[:],
@@ -285,10 +283,20 @@ def tile_cosineattention_pa_kernel(tc, x, w_attn, out_0, out_1, out_2):
                 in1=inv_rms[q][:, j].unsqueeze(1).to_broadcast([P, HEADS, HALF]),
                 op=ALU.mult,
             )
+            finished[q, j] = res
+            if not on_scalar_queue(q, j):
+                store(nc.sync, q, j)
+
+        def on_scalar_queue(q, j):
+            return j == 1 and 2 * THIRDS * GROUPS_PER_PHASE - 8 <= q < GROUPS - 2
+
+        def store(queue, q, j):
+            phase, k = divmod(q, GROUPS_PER_PHASE)
+            third, half = divmod(phase, 2)
             start = GROUP_POSITIONS * k + P * j
+            values = slice(HALF * half, HALF * (half + 1))
             rows = outs[third][:, start : start + P, values].rearrange("n p d -> p n d")
-            queue = nc.gpsimd if q == 18 and j == 0 else nc.sync
-            queue.dma_start(out=rows, in_=res[:])
+            queue.dma_start(out=rows, in_=finished[q, j][:])
 
         load_everything()
         nc.vector.memset(zero_column[:], 0.0)
@@ -387,6 +395,8 @@ def tile_cosineattention_pa_kernel(tc, x, w_attn, out_0, out_1, out_2):
                 quantise_x(5)
             if 0 <= squared < GROUPS and folded_twice(squared):
                 fold_twice(squared)
+            if stored >= 0 and on_scalar_queue(stored, 1):
+                store(nc.scalar, stored, 1)
             if 2 <= q < GROUPS:
                 project(q, 0)
                 project(q, 1)

@@ -32,6 +32,9 @@ BANKS_PER_GROUP = 2
 GROUP_POSITIONS = BANKS_PER_GROUP * P
 GROUPS_PER_PHASE = POSITIONS // GROUP_POSITIONS
 GROUPS = PHASES * GROUPS_PER_PHASE
+DOUBLE_STEP = 17
+LAST_HALF_GROUPS = 3
+FIRST_WHOLE_GROUP = GROUPS - BANKS_PER_GROUP * (GROUPS_PER_PHASE - LAST_HALF_GROUPS)
 X_UNITS = PASSES * GROUPS_PER_PHASE
 FLOPS = 2 * POSITIONS * CHANNELS * THIRDS * HEADS * HEAD_DIM
 
@@ -50,6 +53,7 @@ def tile_cosineattention_pa_kernel(tc, x, w_attn, out_0, out_1, out_2):
         tiny = ctx.enter_context(tc.tile_pool(name="tiny", bufs=3))
         norm = ctx.enter_context(tc.tile_pool(name="norm", bufs=3))
         results = ctx.enter_context(tc.tile_pool(name="results", bufs=12))
+        whole_results = ctx.enter_context(tc.tile_pool(name="whole_results", bufs=2))
         psum = ctx.enter_context(tc.psum_pool(name="psum", bufs=2))
 
         identity = keep.tile([P, P], F32)
@@ -80,6 +84,13 @@ def tile_cosineattention_pa_kernel(tc, x, w_attn, out_0, out_1, out_2):
         folded_squares = {}
         inv_rms = {}
         finished = {}
+
+        members = []
+        for phase in range(PHASES):
+            for k in range(GROUPS_PER_PHASE if phase < PHASES - 2 else LAST_HALF_GROUPS):
+                members.append([(phase, GROUP_POSITIONS * k + P * j) for j in range(BANKS_PER_GROUP)])
+        for start in range(GROUP_POSITIONS * LAST_HALF_GROUPS, POSITIONS, P):
+            members.append([(PHASES - 2 + j, start) for j in range(BANKS_PER_GROUP)])
 
         def load_x(g, first, last):
             rows = x_rows[PACK * P * g : PACK * P * (g + 1), :].rearrange("(p t) s -> p t s", t=PACK)
@@ -190,7 +201,7 @@ def tile_cosineattention_pa_kernel(tc, x, w_attn, out_0, out_1, out_2):
 
         def regroup_filters(b):
             grouped = w_stage.tile([P, PASSES, P, PACK], BF16, align_bytes=64)
-            on_scalar = b < 3 if b < BLOCKS_PER_PHASE else b % 3 == 2 or b >= 20
+            on_scalar = b < 2 if b < BLOCKS_PER_PHASE else b % 3 == 2 or b >= 20
             copy = nc.scalar.copy if on_scalar else nc.vector.tensor_copy
             copy(
                 out=grouped[:]
@@ -212,8 +223,8 @@ def tile_cosineattention_pa_kernel(tc, x, w_attn, out_0, out_1, out_2):
                 )
 
         def project(q, j):
-            phase, k = divmod(q, GROUPS_PER_PHASE)
-            columns = slice(GROUP_POSITIONS * k + P * j, GROUP_POSITIONS * k + P * (j + 1))
+            phase, start = members[q][j]
+            columns = slice(start, start + P)
             bank = psum.tile([P, HEADS, HALF], F32, tag="product", bufs=6)
             for g in range(PASSES):
                 nc.tensor.matmul_mx(
@@ -276,27 +287,26 @@ def tile_cosineattention_pa_kernel(tc, x, w_attn, out_0, out_1, out_2):
             inv_rms[q] = r
 
         def scale_products(q, j):
-            res = results.tile([P, HEADS, HALF], F32)
+            phase, start = members[q][j]
+            third, half = divmod(phase, 2)
+            values = slice(HALF * half, HALF * (half + 1))
+            whole = q >= FIRST_WHOLE_GROUP
+            if whole and j == 0:
+                finished[q] = whole_results.tile([P, HEADS, HEAD_DIM], F32, name="res_whole")
+            res = finished[q][:, :, values] if whole else results.tile([P, HEADS, HALF], F32, name="res")[:]
             nc.vector.tensor_tensor(
-                out=res[:],
+                out=res,
                 in0=products[q, j][:],
                 in1=inv_rms[q][:, j].unsqueeze(1).to_broadcast([P, HEADS, HALF]),
                 op=ALU.mult,
             )
-            finished[q, j] = res
-            if not on_scalar_queue(q, j):
-                store(nc.sync, q, j)
-
-        def on_scalar_queue(q, j):
-            return j == 1 and 2 * THIRDS * GROUPS_PER_PHASE - 8 <= q < GROUPS - 2
-
-        def store(queue, q, j):
-            phase, k = divmod(q, GROUPS_PER_PHASE)
-            third, half = divmod(phase, 2)
-            start = GROUP_POSITIONS * k + P * j
-            values = slice(HALF * half, HALF * (half + 1))
-            rows = outs[third][:, start : start + P, values].rearrange("n p d -> p n d")
-            queue.dma_start(out=rows, in_=finished[q, j][:])
+            rows = outs[third][:, start : start + P, :].rearrange("n p d -> p n d")
+            if not whole:
+                nc.sync.dma_start(out=rows[:, :, values], in_=res)
+            elif j == BANKS_PER_GROUP - 1:
+                for n in range(0, HEADS, HEADS // 2):
+                    heads = slice(n, n + HEADS // 2)
+                    nc.sync.dma_start(out=rows[:, heads], in_=finished[q][:, heads])
 
         load_everything()
         nc.vector.memset(zero_column[:], 0.0)
@@ -310,31 +320,30 @@ def tile_cosineattention_pa_kernel(tc, x, w_attn, out_0, out_1, out_2):
         for b in range(3):
             filter_sum_squares(b)
         filter_inverse_length(0)
-        filter_sum_squares(3)
         filter_floor(0)
         filter_scale(0)
+        filter_sum_squares(3)
         regroup_x(0)
         for b in range(2):
             normalise_filters(b)
             transpose_filters(b)
+        regroup_x(1)
         filter_inverse_length(1)
         filter_floor(1)
         filter_scale(1)
-        regroup_x(1)
+        regroup_filters(0)
         filter_sum_squares(4)
+        quantise_x(0)
         for b in range(2, 4):
             normalise_filters(b)
             transpose_filters(b)
-        regroup_filters(0)
-        regroup_filters(1)
-        quantise_x(0)
         quantise_x(1)
-        regroup_filters(2)
+        regroup_filters(1)
         quantise_filters(0)
+        regroup_filters(2)
         regroup_filters(3)
-        quantise_filters(1)
-        quantise_filters(2)
-        quantise_filters(3)
+        for b in range(1, 4):
+            quantise_filters(b)
         filter_sum_squares(5)
         regroup_x(2)
         regroup_x(3)
@@ -345,18 +354,31 @@ def tile_cosineattention_pa_kernel(tc, x, w_attn, out_0, out_1, out_2):
         quantise_x(3)
         filter_sum_squares(6)
 
+        def blocks_of(q):
+            if q < 0 or q > DOUBLE_STEP + 1:
+                return []
+            b = q + BLOCKS_PER_PHASE + (q > DOUBLE_STEP)
+            return [b, b + 1] if q == DOUBLE_STEP else [b]
+
+        summed = 7
         for q in range(GROUPS + 3):
             squared, added, stored = q - 1, q - 2, q - 3
-            coded, moved, summed = q + 3, q + 4, q + 7
-            pair = (q + 5) // 2 if q % 2 == 1 and q + 5 < BLOCKS else None
+            moved = blocks_of(q)[:1]
+            moved_late = blocks_of(q)[1:]
+            regrouped_late = blocks_of(q - 1)[1:]
+            coded = blocks_of(q - 1)[:1] + blocks_of(q - 2)[1:]
+            pairs = sorted({b // 2 for b in blocks_of(q + 1)} - set(filter_scales))
+            wanted = max([q + 8] + [b + 2 - b % 2 for b in blocks_of(q + 2)])
             if 0 <= squared < GROUPS:
                 square_products(squared, 0)
-            if pair is not None:
+            for pair in pairs:
                 filter_inverse_length(pair)
             if 0 <= squared < GROUPS:
                 square_products(squared, 1)
-            if pair is not None:
+            for pair in pairs:
                 filter_floor(pair)
+            for b in regrouped_late:
+                regroup_filters(b)
             if 0 <= added < GROUPS:
                 add_folded_heads(added)
             if q == 2:
@@ -365,38 +387,43 @@ def tile_cosineattention_pa_kernel(tc, x, w_attn, out_0, out_1, out_2):
             if q < 2:
                 project(q, 0)
                 project(q, 1)
-            if moved < BLOCKS:
-                normalise_filters(moved)
-                transpose_filters(moved)
+            for b in moved:
+                normalise_filters(b)
+                transpose_filters(b)
+            if q == 1:
+                quantise_x(5)
             if 0 <= stored < GROUPS:
                 scale_products(stored, 0)
-            if q > 0 and coded < BLOCKS:
-                quantise_filters(coded)
+            for b in coded:
+                quantise_filters(b)
             if 0 <= stored < GROUPS:
                 scale_products(stored, 1)
-            if summed < BLOCKS:
+            if summed < min(wanted, BLOCKS):
                 filter_sum_squares(summed)
             if 0 <= added < GROUPS:
                 inverse_rms(added)
+            for b in range(summed + 1, min(wanted, BLOCKS)):
+                filter_sum_squares(b)
+            summed = max(summed, min(wanted, BLOCKS))
             if 0 <= squared < GROUPS:
                 fold_heads(squared)
             if q == 0:
                 regroup_x(4)
-                regroup_x(5)
             if q == 2:
                 quantise_x(6)
                 quantise_x(7)
-            if pair is not None:
+            for pair in pairs:
                 filter_scale(pair)
-            if moved < BLOCKS:
-                regroup_filters(moved)
+            for b in moved:
+                regroup_filters(b)
             if q == 0:
+                regroup_x(5)
                 quantise_x(4)
-                quantise_x(5)
             if 0 <= squared < GROUPS and folded_twice(squared):
                 fold_twice(squared)
-            if stored >= 0 and on_scalar_queue(stored, 1):
-                store(nc.scalar, stored, 1)
             if 2 <= q < GROUPS:
                 project(q, 0)
                 project(q, 1)
+            for b in moved_late:
+                normalise_filters(b)
+                transpose_filters(b)

import math
from contextlib import ExitStack

import concourse.masks as masks
import concourse.mybir as mybir

F32 = mybir.dt.float32
BF16 = mybir.dt.bfloat16
U32 = mybir.dt.uint32
U8 = mybir.dt.uint8
FP8X4 = mybir.dt.float8_e4m3fn_x4
ACT = mybir.ActivationFunctionType
ALU = mybir.AluOpType

P = 128
PACK = 4
CHANNELS = 1024
PASSES = CHANNELS // (P * PACK)
POSITIONS = 1024
HEADS = 8
HEAD_DIM = 128
THIRDS = 3
EPS = 1e-4
NORM_FLOOR = EPS * math.sqrt(CHANNELS)
BANK = 512

HALF = HEAD_DIM // 2
PHASES = 2 * THIRDS
BLOCKS_PER_PHASE = HEADS // 2
BLOCKS = PHASES * BLOCKS_PER_PHASE
BANKS_PER_GROUP = 2
GROUP_POSITIONS = BANKS_PER_GROUP * P
GROUPS_PER_PHASE = POSITIONS // GROUP_POSITIONS
GROUPS = PHASES * GROUPS_PER_PHASE
DOUBLE_STEP = 17
LAST_HALF_GROUPS = 3
FIRST_WHOLE_GROUP = GROUPS - BANKS_PER_GROUP * (GROUPS_PER_PHASE - LAST_HALF_GROUPS)
X_UNITS = PASSES * GROUPS_PER_PHASE
FLOPS = 2 * POSITIONS * CHANNELS * THIRDS * HEADS * HEAD_DIM


def tile_cosineattention_pa_kernel(tc, x, w_attn, out_0, out_1, out_2):
    nc = tc.nc
    x_rows = x.rearrange("b c h w -> (b c) (h w)")
    w_halves = w_attn.rearrange("(t j i h d) c a b -> t h i d j (c a b)", t=THIRDS, i=2, h=2, d=HALF)
    outs = [o.rearrange("b n s d -> (b n) s d") for o in (out_0, out_1, out_2)]

    with ExitStack() as ctx:
        ctx.enter_context(tc.manual_schedule())
        keep = ctx.enter_context(tc.tile_pool(name="keep", bufs=1))
        x_stage = ctx.enter_context(tc.tile_pool(name="x_stage", bufs=3))
        w_stage = ctx.enter_context(tc.tile_pool(name="w_stage", bufs=3))
        tiny = ctx.enter_context(tc.tile_pool(name="tiny", bufs=3))
        norm = ctx.enter_context(tc.tile_pool(name="norm", bufs=3))
        results = ctx.enter_context(tc.tile_pool(name="results", bufs=12))
        whole_results = ctx.enter_context(tc.tile_pool(name="whole_results", bufs=2))
        psum = ctx.enter_context(tc.psum_pool(name="psum", bufs=2))

        identity = keep.tile([P, P], F32)
        deal = keep.tile([P, 2, HALF], F32)
        zero_column = keep.tile([P, 1], F32)
        eps_column = keep.tile([P, 1], F32)
        table_warmer = keep.tile([P, 1], F32)
        tiny_column = keep.tile([P, 1], F32)
        one_column = keep.tile([P, 1], F32)
        x_codes = keep.tile([P, PASSES, POSITIONS], U32, align_bytes=256)
        x_scales = keep.tile([P, PASSES, POSITIONS], U8, align_bytes=256)
        w_codes = keep.tile([P, PHASES, PASSES, BANK], U32, align_bytes=256)
        w_scales = keep.tile([P, PHASES, PASSES, BANK], U8, align_bytes=256)

        x_raw = {}
        w_raw = {}
        sum_squares = {}
        inverse_lengths = {}
        padded_lengths = {}
        filter_scales = {}
        normed = {}
        turned = {}
        grouped_w = {}
        grouped_x = {}
        products = {}
        squares = {}
        head_sums = {}
        folded_squares = {}
        inv_rms = {}
        finished = {}

        members = []
        for phase in range(PHASES):
            for k in range(GROUPS_PER_PHASE if phase < PHASES - 2 else LAST_HALF_GROUPS):
                members.append([(phase, GROUP_POSITIONS * k + P * j) for j in range(BANKS_PER_GROUP)])
        for start in range(GROUP_POSITIONS * LAST_HALF_GROUPS, POSITIONS, P):
            members.append([(PHASES - 2 + j, start) for j in range(BANKS_PER_GROUP)])

        def load_x(g, first, last):
            rows = x_rows[PACK * P * g : PACK * P * (g + 1), :].rearrange("(p t) s -> p t s", t=PACK)
            raw = keep.tile([P, PACK, GROUP_POSITIONS * (last - first)], BF16, name="x_%d_%d" % (g, first))
            nc.sync.dma_start(out=raw[:], in_=rows[:, :, GROUP_POSITIONS * first : GROUP_POSITIONS * last])
            for k in range(first, last):
                x_raw[k, g] = raw[:, :, GROUP_POSITIONS * (k - first) : GROUP_POSITIONS * (k - first + 1)]

        def load_filters(phase, first, last):
            third, half = divmod(phase, 2)
            raw = keep.tile([P, last - first, CHANNELS], BF16, name="w_%d_%d" % (phase, first))
            for i in range(2):
                nc.sync.dma_start(out=raw[i:P:2], in_=w_halves[third, half, i, :, first:last, :])
            for j in range(first, last):
                w_raw[BLOCKS_PER_PHASE * phase + j] = raw[:, j - first, :]

        def load_everything():
            for j in range(BLOCKS_PER_PHASE):
                load_filters(0, j, j + 1)
            for g in range(PASSES):
                load_x(g, 0, 1)
            load_filters(1, 0, 1)
            load_filters(1, 1, 2)
            for g in range(PASSES):
                load_x(g, 1, 2)
            load_filters(1, 2, 4)
            for g in range(PASSES):
                load_x(g, 2, 4)
            for phase in range(2, PHASES):
                load_filters(phase, 0, 2)
                load_filters(phase, 2, 4)

        def regroup_x(unit):
            k, g = divmod(unit, PASSES)
            grouped = x_stage.tile([P, GROUP_POSITIONS, PACK], BF16, align_bytes=64)
            rows = x_raw[k, g]
            nc.vector.tensor_copy(
                out=grouped[:].rearrange("p (c i) t -> p c t i", i=4),
                in_=rows.rearrange("p t (c i) -> p c t i", i=4),
            )
            grouped_x[unit] = grouped

        def quantise_x(unit):
            k, g = divmod(unit, PASSES)
            columns = slice(GROUP_POSITIONS * k, GROUP_POSITIONS * (k + 1))
            nc.vector.quantize_mx(
                out=x_codes[:, g, columns].bitcast(FP8X4),
                scales=x_scales[:, g, columns],
                in_=grouped_x[unit][:].rearrange("p s t -> p (s t)"),
            )

        def filter_sum_squares(b):
            pair, member = divmod(b, 2)
            if member == 0:
                sum_squares[pair] = tiny.tile([P, 2], F32, name="totals")
            unread = w_stage.tile([P, CHANNELS], BF16)
            total = sum_squares[pair][:, member : member + 1]
            if b == 1:
                nc.vector.scalar_tensor_tensor(
                    out=unread[:], in0=w_raw[b], scalar=1.0, in1=w_raw[b], op0=ALU.mult, op1=ALU.mult, accum_out=total
                )
            else:
                nc.scalar.activation(out=unread[:], in_=w_raw[b], func=ACT.Square, accum_out=total)

        def filter_inverse_length(pair):
            inverse = tiny.tile([P, 2], F32)
            nc.scalar.activation(
                out=inverse[:], in_=sum_squares[pair][:], func=ACT.Abs_reciprocal_sqrt, bias=tiny_column[:]
            )
            inverse_lengths[pair] = inverse

        def filter_floor(pair):
            padded = tiny.tile([P, 2], F32)
            nc.scalar.activation(
                out=padded[:], in_=inverse_lengths[pair][:], func=ACT.Identity, scale=NORM_FLOOR, bias=one_column[:]
            )
            padded_lengths[pair] = padded

        def filter_scale(pair):
            scales = tiny.tile([P, 2], F32)
            nc.vector.reciprocal(out=scales[:], in_=padded_lengths[pair][:])
            filter_scales[pair] = scales

        def normalise_filters(b):
            pair, member = divmod(b, 2)
            wn = w_stage.tile([P, 2, CHANNELS // PACK, 2], BF16)
            nc.vector.tensor_scalar(
                out=wn[:],
                in0=w_raw[b].rearrange("o (r u e) -> o u r e", u=2, e=2),
                scalar1=inverse_lengths[pair][:, member : member + 1],
                scalar2=filter_scales[pair][:, member : member + 1],
                op0=ALU.mult,
                op1=ALU.mult,
            )
            normed[b] = wn

        def transpose_filters(b):
            words = normed[b][:].rearrange("o u r e -> o (u r e)").bitcast(F32)
            first = b < BLOCKS_PER_PHASE
            bank = psum.tile(
                [P, PASSES * 2, P], F32, tag="product" if first else "turned", bufs=6 if first else 1
            )
            for c in range(PASSES * 2):
                g, u = divmod(c, 2)
                start = P * (PASSES * u + g)
                nc.tensor.transpose(bank[:, c, :], words[:, start : start + P], deal[:].rearrange("p i d -> p (i d)"))
            turned[b] = bank

        def regroup_filters(b):
            grouped = w_stage.tile([P, PASSES, P, PACK], BF16, align_bytes=64)
            on_scalar = b < 2 if b < BLOCKS_PER_PHASE else b % 3 == 2 or b >= 20
            copy = nc.scalar.copy if on_scalar else nc.vector.tensor_copy
            copy(
                out=grouped[:]
                .rearrange("p g o t -> p (g o t)")
                .bitcast(F32)
                .rearrange("p (g o u) -> p g o u", g=PASSES, u=2),
                in_=turned[b][:].rearrange("p (g u) o -> p g o u", u=2),
            )
            grouped_w[b] = grouped

        def quantise_filters(b):
            phase, j = divmod(b, BLOCKS_PER_PHASE)
            columns = slice(P * j, P * (j + 1))
            for g in range(PASSES):
                nc.vector.quantize_mx(
                    out=w_codes[:, phase, g, columns].bitcast(FP8X4),
                    scales=w_scales[:, phase, g, columns],
                    in_=grouped_w[b][:, g].rearrange("p o t -> p (o t)"),
                )

        def project(q, j):
            phase, start = members[q][j]
            columns = slice(start, start + P)
            bank = psum.tile([P, HEADS, HALF], F32, tag="product", bufs=6)
            for g in range(PASSES):
                nc.tensor.matmul_mx(
                    out=bank[:].rearrange("p n d -> p (n d)"),
                    lhsT=x_codes[:, g, columns].bitcast(FP8X4),
                    lhsT_scale=x_scales[:, g, columns],
                    rhs=w_codes[:, phase, g, :].bitcast(FP8X4),
                    rhs_scale=w_scales[:, phase, g, :],
                    start=(g == 0),
                    stop=(g == PASSES - 1),
                )
            products[q, j] = bank

        def square_products(q, j):
            if j == 0:
                squares[q] = norm.tile([P, HEADS, BANKS_PER_GROUP, HALF], F32, name="sq")
            nc.scalar.activation(out=squares[q][:, :, j, :], in_=products[q, j][:], func=ACT.Square)

        def fold_heads(q):
            four = norm.tile([P, HEADS // 2, P], F32)
            eight = squares[q][:].rearrange("p n j d -> p n (j d)")
            nc.vector.tensor_tensor(
                out=four[:], in0=eight[:, : HEADS // 2], in1=eight[:, HEADS // 2 :], op=ALU.add
            )
            folded_squares[q] = four

        def fold_twice(q):
            two = norm.tile([P, HEADS // 4, P], F32)
            four = folded_squares[q]
            nc.vector.tensor_tensor(
                out=two[:], in0=four[:, : HEADS // 4], in1=four[:, HEADS // 4 :], op=ALU.add
            )
            folded_squares[q] = two

        def folded_twice(q):
            return q >= 17 and q % 2 == 1

        def add_folded_heads(q):
            total = psum.tile([P, P], F32, tag="head_sum", bufs=1)
            left = HEADS // 4 if folded_twice(q) else HEADS // 2
            for n in range(left):
                nc.tensor.matmul(
                    out=total[:],
                    lhsT=identity[:],
                    rhs=folded_squares[q][:, n],
                    start=(n == 0),
                    stop=(n == left - 1),
                )
            head_sums[q] = total

        def inverse_rms(q):
            r = norm.tile([P, BANKS_PER_GROUP, HALF], F32)
            nc.scalar.activation(
                out=r[:].rearrange("p j d -> p (j d)"),
                in_=head_sums[q][:],
                func=ACT.Abs_reciprocal_sqrt,
                scale=1.0 / HEADS,
                bias=eps_column[:],
            )
            inv_rms[q] = r

        def scale_products(q, j):
            phase, start = members[q][j]
            third, half = divmod(phase, 2)
            values = slice(HALF * half, HALF * (half + 1))
            whole = q >= FIRST_WHOLE_GROUP
            if whole and j == 0:
                finished[q] = whole_results.tile([P, HEADS, HEAD_DIM], F32, name="res_whole")
            res = finished[q][:, :, values] if whole else results.tile([P, HEADS, HALF], F32, name="res")[:]
            nc.vector.tensor_tensor(
                out=res,
                in0=products[q, j][:],
                in1=inv_rms[q][:, j].unsqueeze(1).to_broadcast([P, HEADS, HALF]),
                op=ALU.mult,
            )
            rows = outs[third][:, start : start + P, :].rearrange("n p d -> p n d")
            if not whole:
                nc.sync.dma_start(out=rows[:, :, values], in_=res)
            elif j == BANKS_PER_GROUP - 1:
                for n in range(0, HEADS, HEADS // 2):
                    heads = slice(n, n + HEADS // 2)
                    nc.sync.dma_start(out=rows[:, heads], in_=finished[q][:, heads])

        load_everything()
        nc.vector.memset(zero_column[:], 0.0)
        nc.vector.tensor_scalar_add(out=eps_column[:], in0=zero_column[:], scalar1=EPS)
        nc.vector.memset(one_column[:], 1.0)
        nc.vector.tensor_scalar_add(out=tiny_column[:], in0=zero_column[:], scalar1=1e-30)
        nc.scalar.activation(out=table_warmer[:], in_=eps_column[:], func=ACT.Abs_reciprocal_sqrt)
        masks.make_identity(nc, identity[:])
        nc.vector.tensor_copy(out=deal[:], in_=identity[:].rearrange("p (d i) -> p i d", i=2))

        for b in range(3):
            filter_sum_squares(b)
        filter_inverse_length(0)
        filter_floor(0)
        filter_scale(0)
        filter_sum_squares(3)
        regroup_x(0)
        for b in range(2):
            normalise_filters(b)
            transpose_filters(b)
        regroup_x(1)
        filter_inverse_length(1)
        filter_floor(1)
        filter_scale(1)
        regroup_filters(0)
        filter_sum_squares(4)
        quantise_x(0)
        for b in range(2, 4):
            normalise_filters(b)
            transpose_filters(b)
        quantise_x(1)
        regroup_filters(1)
        quantise_filters(0)
        regroup_filters(2)
        regroup_filters(3)
        for b in range(1, 4):
            quantise_filters(b)
        filter_sum_squares(5)
        regroup_x(2)
        regroup_x(3)
        filter_inverse_length(2)
        filter_floor(2)
        filter_scale(2)
        quantise_x(2)
        quantise_x(3)
        filter_sum_squares(6)

        def blocks_of(q):
            if q < 0 or q > DOUBLE_STEP + 1:
                return []
            b = q + BLOCKS_PER_PHASE + (q > DOUBLE_STEP)
            return [b, b + 1] if q == DOUBLE_STEP else [b]

        summed = 7
        for q in range(GROUPS + 3):
            squared, added, stored = q - 1, q - 2, q - 3
            moved = blocks_of(q)[:1]
            moved_late = blocks_of(q)[1:]
            regrouped_late = blocks_of(q - 1)[1:]
            coded = blocks_of(q - 1)[:1] + blocks_of(q - 2)[1:]
            pairs = sorted({b // 2 for b in blocks_of(q + 1)} - set(filter_scales))
            wanted = max([q + 8] + [b + 2 - b % 2 for b in blocks_of(q + 2)])
            if 0 <= squared < GROUPS:
                square_products(squared, 0)
            for pair in pairs:
                filter_inverse_length(pair)
            if 0 <= squared < GROUPS:
                square_products(squared, 1)
            for pair in pairs:
                filter_floor(pair)
            for b in regrouped_late:
                regroup_filters(b)
            if 0 <= added < GROUPS:
                add_folded_heads(added)
            if q == 2:
                regroup_x(6)
                regroup_x(7)
            if q < 2:
                project(q, 0)
                project(q, 1)
            for b in moved:
                normalise_filters(b)
                transpose_filters(b)
            if q == 1:
                quantise_x(5)
            if 0 <= stored < GROUPS:
                scale_products(stored, 0)
            for b in coded:
                quantise_filters(b)
            if 0 <= stored < GROUPS:
                scale_products(stored, 1)
            if summed < min(wanted, BLOCKS):
                filter_sum_squares(summed)
            if 0 <= added < GROUPS:
                inverse_rms(added)
            for b in range(summed + 1, min(wanted, BLOCKS)):
                filter_sum_squares(b)
            summed = max(summed, min(wanted, BLOCKS))
            if 0 <= squared < GROUPS:
                fold_heads(squared)
            if q == 0:
                regroup_x(4)
            if q == 2:
                quantise_x(6)
                quantise_x(7)
            for pair in pairs:
                filter_scale(pair)
            for b in moved:
                regroup_filters(b)
            if q == 0:
                regroup_x(5)
                quantise_x(4)
            if 0 <= squared < GROUPS and folded_twice(squared):
                fold_twice(squared)
            if 2 <= q < GROUPS:
                project(q, 0)
                project(q, 1)
            for b in moved_late:
                normalise_filters(b)
                transpose_filters(b)
